import numpy as np
import ml_dtypes


def mxq(x, axis, fmt="e4m3"):
    dtype, down = {"e4m3": (ml_dtypes.float8_e4m3fn, 7), "e5m2": (ml_dtypes.float8_e5m2, 14)}[fmt]
    v = np.moveaxis(np.asarray(x, np.float32).astype(ml_dtypes.bfloat16).astype(np.float64), axis, -1)
    blocks = v.reshape(v.shape[:-1] + (-1, 32))
    amax = np.abs(blocks).max(-1, keepdims=True)
    byte = np.maximum(np.where(amax > 0, np.frexp(amax)[1] - 1 + 127, 0) - down, 1)
    scale = np.exp2(byte - 127.0)
    codes = (blocks / scale).astype(np.float32).astype(dtype).astype(np.float64)
    return np.moveaxis((codes * scale).reshape(v.shape), -1, axis)


WIDE = False


def mx_kscale(k):
    if not WIDE:
        return np.ones(k)
    levels = np.array([10, -10, 5, -5, 0])
    a = np.random.permutation(np.resize(levels, k // 512 * 4)).reshape(k // 512, 4)
    idx = np.arange(k)
    return np.exp2(a[idx // 512, idx % 128 // 32])


BF16 = ml_dtypes.bfloat16


def bf(x):
    return np.asarray(x, np.float32).astype(BF16)


def f64(x):
    return np.asarray(x).astype(np.float64)


E2M1 = np.array([0.0, 0.5, 1.0, 1.5, 2.0, 3.0, 4.0, 6.0, -0.0, -0.5, -1.0, -1.5, -2.0, -3.0, -4.0, -6.0])


def pack_weight(w, fmt):
    k, n = w.shape
    w = f64(bf(w)).reshape(k // 32, 32, n)
    amax = np.abs(w).max(1)
    if fmt == "e4m3":
        byte = np.frexp(amax)[1] - 1 + 127 - 7
    else:
        mant, ex = np.frexp(amax / 6.0)
        byte = np.where(mant > 0.5, ex, ex - 1) + 127
    byte = np.clip(np.where(amax > 0, byte, 1), 1, 254)
    scaled = (w * np.exp2(127.0 - byte)[:, None, :]).reshape(k, n).astype(np.float32)
    by_word = np.ascontiguousarray(scaled.reshape(k // 512, 128, 4, n).transpose(0, 1, 3, 2))
    if fmt == "e4m3":
        words = by_word.astype(ml_dtypes.float8_e4m3fn).view(np.uint8)
    else:
        c = by_word.astype(ml_dtypes.float4_e2m1fn).view(np.uint8) & 0xF
        words = c[..., 0::2] | (c[..., 1::2] << 4)
    return np.ascontiguousarray(words), np.ascontiguousarray(byte.astype(np.uint8).reshape(k // 512, 16, n))


def unpack_weight(words, scales, fmt):
    g, p, n, _ = words.shape
    if fmt == "e4m3":
        vals = np.ascontiguousarray(words).view(ml_dtypes.float8_e4m3fn).astype(np.float64)
    else:
        nib = np.empty((g, p, n, 4), np.uint8)
        nib[..., 0::2] = words & 0xF
        nib[..., 1::2] = words >> 4
        vals = E2M1[nib]
    vals = vals * np.repeat(np.exp2(scales.astype(np.float64) - 127.0), 8, axis=1)[..., None]
    return vals.transpose(0, 1, 3, 2).reshape(g * 512, n)


B, F, DEPTH, T, DO = 2048, 512, 6, 64, 128
L = 2 ** DEPTH


def sigmoid(v):
    return 1.0 / (1.0 + np.exp(-v))


def setup_inputs():
    s = mx_kscale(F)
    x = bf(np.random.standard_normal((B, F)) * s)
    W = np.random.standard_normal((DEPTH, F, T)) * 1.5 / np.sqrt(F) / s[None, :, None]
    W_words, W_scales = pack_weight(W.reshape(-1, T), "e4m3")
    b = bf(np.random.standard_normal((DEPTH, T)) * 0.5)
    leaf_values = bf(np.random.standard_normal((T, L, DO)) * np.sqrt(T))
    return {"x": x,
            "W_words": W_words,
            "W_scales": W_scales,
            "b": b,
            "leaf_values": leaf_values}


def reference(x, W_words, W_scales, b, leaf_values):
    z = mxq(f64(x), 1, "e4m3") @ unpack_weight(W_words, W_scales, "e4m3").reshape(DEPTH, F, T)
    split_probs = sigmoid(z.transpose(1, 0, 2) + f64(b))
    leaf_ids = np.arange(L)
    path_probs = np.ones((x.shape[0], T, L))
    for level in range(DEPTH):
        bit = (leaf_ids >> (DEPTH - level - 1)) & 1
        p = split_probs[:, level, :, None]
        path_probs = path_probs * np.where(bit == 0, p, 1.0 - p)
    pq = mxq(path_probs.reshape(-1, T * L), 1, "e4m3")
    lq = mxq(f64(leaf_values).reshape(T * L, DO), 0, "e4m3")
    return (pq @ lq) / T

@@ -1,0 +1,240 @@
+from contextlib import ExitStack
+
+import concourse.mybir as mybir
+from concourse.masks import make_identity
+
+F32 = mybir.dt.float32
+BF16 = mybir.dt.bfloat16
+I32 = mybir.dt.int32
+U32 = mybir.dt.uint32
+U8 = mybir.dt.uint8
+FP8X4 = mybir.dt.float8_e4m3fn_x4
+MULT = mybir.AluOpType.mult
+SIGMOID = mybir.ActivationFunctionType.Sigmoid
+COPY = mybir.ActivationFunctionType.Copy
+
+P = 128
+PACK = 4
+BATCH, FEATURES, DEPTH, TREES, LEAVES, D_OUT = 2048, 512, 6, 64, 64, 128
+PASSES = TREES * LEAVES // (P * PACK)
+N_TILES = BATCH // P
+CHUNK_TILES = 4
+CHUNK = CHUNK_TILES * P
+N_CHUNKS = N_TILES // CHUNK_TILES
+
+FLOPS = 2 * BATCH * FEATURES * DEPTH * TREES + 2 * BATCH * TREES * LEAVES * D_OUT
+
+
+def tile_neuralobliviousdecisiontree_e_kernel(tc, x, W_words, W_scales, b, leaf_values, out):
+    nc = tc.nc
+    with ExitStack() as ctx:
+        const = ctx.enter_context(tc.tile_pool(name="const", bufs=1))
+        x_pool = ctx.enter_context(tc.tile_pool(name="x_pool", bufs=2))
+        factor_pool = ctx.enter_context(tc.tile_pool(name="factor_pool", bufs=2))
+        path_pool = ctx.enter_context(tc.tile_pool(name="path_pool", bufs=3))
+        out_pool = ctx.enter_context(tc.tile_pool(name="out_pool", bufs=2))
+        psum = ctx.enter_context(tc.psum_pool(name="psum", bufs=2))
+
+        x_rows = x.rearrange("(p c) f -> p c f", c=N_TILES)
+        out_rows = out.rearrange("(p c) d -> p c d", c=N_TILES)
+        x_raw = []
+        for q in range(N_CHUNKS):
+            x_raw.append(const.tile([P, CHUNK_TILES, FEATURES], BF16, name="x_raw%d" % q))
+        nc.sync.dma_start(out=x_raw[0][:], in_=x_rows[:, 0:CHUNK_TILES, :])
+
+        w_codes = const.tile([P, DEPTH, 2, TREES], U32, align_bytes=64)
+        w_scales = const.tile([P, DEPTH, 2, TREES], U8, align_bytes=64)
+        nc.vector.memset(w_scales[:].rearrange("p j h t -> p (j h t)").bitcast(I32), 0)
+        nc.sync.dma_start(
+            out=w_codes[:, :, 0, :].bitcast(I32),
+            in_=W_words.rearrange("j p t e -> p j (t e)").bitcast(I32),
+        )
+        scale_rows = W_scales.rearrange("j s t -> s j t").bitcast(I32)
+        for quadrant in range(4):
+            nc.sync.dma_start(
+                out=w_scales[32 * quadrant : 32 * quadrant + 4, :, 0, :].bitcast(I32),
+                in_=scale_rows[4 * quadrant : 4 * quadrant + 4, :, :],
+            )
+        for q in range(1, N_CHUNKS):
+            nc.sync.dma_start(out=x_raw[q][:], in_=x_rows[:, q * CHUNK_TILES : (q + 1) * CHUNK_TILES, :])
+        nc.vector.tensor_copy(out=w_codes[:, :, 1, :].bitcast(I32), in_=w_codes[:, :, 0, :].bitcast(I32))
+        nc.vector.tensor_copy(out=w_scales[:, :, 1, :].bitcast(I32), in_=w_scales[:, :, 0, :].bitcast(I32))
+
+        b_rows = const.tile([P, P], BF16)
+        nc.vector.memset(b_rows[:], 0.0)
+        leaf_raw = const.tile([P, LEAVES // 2, D_OUT], BF16)
+        for b0 in range(2):
+            nc.scalar.dma_start(out=b_rows[0:DEPTH, TREES * b0 : TREES * (b0 + 1)], in_=b)
+        for b0 in range(2):
+            nc.scalar.dma_start(
+                out=leaf_raw[TREES * b0 : TREES * (b0 + 1), :, :],
+                in_=leaf_values[:, (LEAVES // 2) * b0 : (LEAVES // 2) * (b0 + 1), :],
+            )
+
+        ident = const.tile([P, P], F32)
+        make_identity(nc, ident[:])
+        half_sign = const.tile([P, 1], F32)
+        nc.vector.memset(half_sign[0:TREES, :], 1.0)
+        nc.vector.memset(half_sign[TREES:P, :], -1.0)
+        table_warmer = const.tile([P, 1], F32)
+        nc.scalar.activation(out=table_warmer[:], in_=half_sign[:], func=SIGMOID)
+
+        b_rows_f32 = const.tile([P, P], F32)
+        nc.vector.tensor_copy(out=b_rows_f32[:], in_=b_rows[:])
+        b_cols = psum.tile([P, P], F32, tag="x_t")
+        nc.tensor.transpose(out=b_cols[:], in_=b_rows_f32[:], identity=ident[:])
+        bias_keep = const.tile([P, DEPTH], F32)
+        bias_flip = const.tile([P, DEPTH], F32)
+        half_bias = const.tile([P, 1], F32)
+        nc.vector.tensor_copy(out=bias_keep[:], in_=b_cols[:, 0:DEPTH])
+        nc.vector.tensor_scalar_mul(out=bias_flip[:], in0=b_cols[:, 0:DEPTH], scalar1=-1.0)
+        nc.vector.tensor_tensor(out=half_bias[:], in0=bias_keep[:, 0:1], in1=half_sign[:], op=MULT)
+
+        leaf_grouped = const.tile([P, PASSES, D_OUT, PACK], BF16, align_bytes=64)
+        leaf_codes = const.tile([P, PASSES, D_OUT], U32, align_bytes=64)
+        leaf_scales = const.tile([P, PASSES, D_OUT], U8, align_bytes=64)
+        nc.vector.tensor_copy(out=leaf_grouped[:], in_=leaf_raw[:].rearrange("p (g j) d -> p g d j", j=PACK))
+        nc.vector.quantize_mx(
+            out=leaf_codes[:].rearrange("p g d -> p (g d)").bitcast(FP8X4),
+            scales=leaf_scales[:].rearrange("p g d -> p (g d)"),
+            in_=leaf_grouped[:].rearrange("p g d j -> p (g d j)"),
+        )
+
+        upper = {}
+        lower = {}
+
+        def split_probabilities(q):
+            x_words = x_raw[q][:].rearrange("p c f -> p (c f)").bitcast(F32)
+            words_per_row = FEATURES // 2
+            x_grouped = x_pool.tile([P, CHUNK * PACK], BF16, align_bytes=64)
+            grouped_words = x_grouped[:].bitcast(F32).rearrange("p (c n u) -> p c n u", c=CHUNK_TILES, u=2)
+            for pair in range(CHUNK_TILES // 2):
+                x_t = psum.tile([P, 2, 2, P], F32, tag="x_t")
+                for i in range(2):
+                    first = (2 * pair + i) * words_per_row
+                    for u in range(2):
+                        nc.tensor.transpose(
+                            out=x_t[:, i, u, :],
+                            in_=x_words[:, first + u : first + words_per_row : 2],
+                            identity=ident[:],
+                        )
+                nc.scalar.copy(
+                    out=grouped_words[:, 2 * pair : 2 * pair + 2, :, :],
+                    in_=x_t[:].rearrange("p c u n -> p c n u"),
+                )
+            x_codes = x_pool.tile([P, CHUNK], U32, align_bytes=64)
+            x_scales = x_pool.tile([P, CHUNK], U8, align_bytes=64)
+            nc.vector.quantize_mx(out=x_codes[:].bitcast(FP8X4), scales=x_scales[:], in_=x_grouped[:])
+
+            factors = []
+            for level in range(DEPTH):
+                z = psum.tile([P, CHUNK], F32, tag="z")
+                nc.tensor.matmul_mx(
+                    out=z[:],
+                    lhsT=w_codes[:, level, :, :].rearrange("p h t -> p (h t)").bitcast(FP8X4),
+                    lhsT_scale=w_scales[:, level, :, :].rearrange("p h t -> p (h t)"),
+                    rhs=x_codes[:].bitcast(FP8X4),
+                    rhs_scale=x_scales[:],
+                    start=True,
+                    stop=True,
+                )
+                if level == 0:
+                    f = factor_pool.tile([P, CHUNK], F32, name="f0")
+                    nc.scalar.activation(out=f[:], in_=z[:], func=SIGMOID, bias=half_bias[:], scale=half_sign[:])
+                else:
+                    f = factor_pool.tile([P, 2, CHUNK], F32, name="f%d" % level)
+                    nc.scalar.activation(
+                        out=f[:, 0, :], in_=z[:], func=SIGMOID, bias=bias_keep[:, level : level + 1], scale=1.0
+                    )
+                    nc.scalar.activation(
+                        out=f[:, 1, :], in_=z[:], func=SIGMOID, bias=bias_flip[:, level : level + 1], scale=-1.0
+                    )
+                factors.append(f)
+
+            eng = nc.vector if q == 0 else nc.gpsimd
+            f0, f1, f2, f3, f4, f5 = factors
+            c4 = factor_pool.tile([P, CHUNK, 2, 2], F32, name="c4")
+            eng.tensor_tensor(
+                out=c4[:],
+                in0=f4[:].rearrange("p b n -> p n b").unsqueeze(3).to_broadcast([P, CHUNK, 2, 2]),
+                in1=f5[:].rearrange("p b n -> p n b").unsqueeze(2).to_broadcast([P, CHUNK, 2, 2]),
+                op=MULT,
+            )
+            a2 = factor_pool.tile([P, 2, CHUNK], F32, name="a2")
+            eng.tensor_tensor(out=a2[:], in0=f0[:].unsqueeze(1).to_broadcast([P, 2, CHUNK]), in1=f1[:], op=MULT)
+            a4 = factor_pool.tile([P, 2, 2, CHUNK], F32, name="a4")
+            eng.tensor_tensor(
+                out=a4[:],
+                in0=a2[:].unsqueeze(2).to_broadcast([P, 2, 2, CHUNK]),
+                in1=f2[:].unsqueeze(1).to_broadcast([P, 2, 2, CHUNK]),
+                op=MULT,
+            )
+            a8 = factor_pool.tile([P, 4, 2, CHUNK], F32, name="a8")
+            eng.tensor_tensor(
+                out=a8[:],
+                in0=a4[:].rearrange("p a b n -> p (a b) n").unsqueeze(2).to_broadcast([P, 4, 2, CHUNK]),
+                in1=f3[:].unsqueeze(1).to_broadcast([P, 4, 2, CHUNK]),
+                op=MULT,
+            )
+            upper[q] = a8[:].rearrange("p a b n -> p (a b) n")
+            lower[q] = c4[:].rearrange("p n a b -> p n (a b)")
+
+        paths = {}
+
+        def multiply(t):
+            q, i = divmod(t, CHUNK_TILES)
+            columns = slice(i * P, (i + 1) * P)
+            lower_ps = psum.tile([P, P, PACK], F32, tag="lower_ps")
+            nc.tensor.matmul(
+                out=lower_ps[:].rearrange("p n j -> p (n j)"),
+                lhsT=ident[:],
+                rhs=lower[q][:, columns, :].rearrange("p n j -> p (n j)"),
+                start=True,
+                stop=True,
+            )
+            path = path_pool.tile([P, PASSES, P, PACK], BF16, align_bytes=64)
+            nc.vector.tensor_tensor(
+                out=path[:],
+                in0=upper[q][:, :, columns].unsqueeze(3).to_broadcast([P, PASSES, P, PACK]),
+                in1=lower_ps[:].unsqueeze(1).to_broadcast([P, PASSES, P, PACK]),
+                op=MULT,
+            )
+            paths[t] = path
+
+        results = {}
+
+        def contract(t):
+            q, i = divmod(t, CHUNK_TILES)
+            path_codes = path_pool.tile([P, PASSES, P], U32, align_bytes=64)
+            path_scales = path_pool.tile([P, PASSES, P], U8, align_bytes=64)
+            nc.vector.quantize_mx(
+                out=path_codes[:].rearrange("p g n -> p (g n)").bitcast(FP8X4),
+                scales=path_scales[:].rearrange("p g n -> p (g n)"),
+                in_=paths[t][:].rearrange("p g n j -> p (g n j)"),
+            )
+            acc = psum.tile([P, D_OUT], F32, tag="acc")
+            for g in range(PASSES):
+                nc.tensor.matmul_mx(
+                    out=acc[:],
+                    lhsT=path_codes[:, g, :].bitcast(FP8X4),
+                    lhsT_scale=path_scales[:, g, :],
+                    rhs=leaf_codes[:, g, :].bitcast(FP8X4),
+                    rhs_scale=leaf_scales[:, g, :],
+                    start=(g == 0),
+                    stop=(g == PASSES - 1),
+                )
+            if i == 0:
+                results[q] = out_pool.tile([P, CHUNK_TILES, D_OUT], F32, name="result")
+            nc.scalar.activation(out=results[q][:, i, :], in_=acc[:], func=COPY, scale=1.0 / TREES)
+            if i == CHUNK_TILES - 1:
+                nc.sync.dma_start(out=out_rows[:, q * CHUNK_TILES : (q + 1) * CHUNK_TILES, :], in_=results[q][:])
+
+        split_probabilities(0)
+        for t in range(N_TILES):
+            q, i = divmod(t, CHUNK_TILES)
+            if i == 0 and q + 1 < N_CHUNKS:
+                split_probabilities(q + 1)
+            multiply(t)
+            if t >= 1:
+                contract(t - 1)
+        contract(N_TILES - 1)

@@ -21,6 +21,7 @@ N_TILES = BATCH // P
 CHUNK_TILES = 4
 CHUNK = CHUNK_TILES * P
 N_CHUNKS = N_TILES // CHUNK_TILES
+LEVEL_ORDER = (4, 5, 0, 1, 2, 3)
 
 FLOPS = 2 * BATCH * FEATURES * DEPTH * TREES + 2 * BATCH * TREES * LEAVES * D_OUT
 
@@ -28,6 +29,7 @@ FLOPS = 2 * BATCH * FEATURES * DEPTH * TREES + 2 * BATCH * TREES * LEAVES * D_OU
 def tile_neuralobliviousdecisiontree_e_kernel(tc, x, W_words, W_scales, b, leaf_values, out):
     nc = tc.nc
     with ExitStack() as ctx:
+        ctx.enter_context(tc.manual_schedule())
         const = ctx.enter_context(tc.tile_pool(name="const", bufs=1))
         x_pool = ctx.enter_context(tc.tile_pool(name="x_pool", bufs=2))
         factor_pool = ctx.enter_context(tc.tile_pool(name="factor_pool", bufs=2))
@@ -40,11 +42,20 @@ def tile_neuralobliviousdecisiontree_e_kernel(tc, x, W_words, W_scales, b, leaf_
         x_raw = []
         for q in range(N_CHUNKS):
             x_raw.append(const.tile([P, CHUNK_TILES, FEATURES], BF16, name="x_raw%d" % q))
-        nc.sync.dma_start(out=x_raw[0][:], in_=x_rows[:, 0:CHUNK_TILES, :])
+
+        def load_x(q):
+            nc.sync.dma_start(out=x_raw[q][:], in_=x_rows[:, q * CHUNK_TILES : (q + 1) * CHUNK_TILES, :])
 
         w_codes = const.tile([P, DEPTH, 2, TREES], U32, align_bytes=64)
         w_scales = const.tile([P, DEPTH, 2, TREES], U8, align_bytes=64)
+        b_rows = const.tile([P, P], BF16)
+        leaf_raw = const.tile([P, LEAVES // 2, D_OUT], BF16)
         nc.vector.memset(w_scales[:].rearrange("p j h t -> p (j h t)").bitcast(I32), 0)
+        nc.vector.memset(b_rows[:], 0.0)
+        for b0 in range(2):
+            nc.scalar.dma_start(out=b_rows[0:DEPTH, TREES * b0 : TREES * (b0 + 1)], in_=b)
+        load_x(0)
+        load_x(1)
         nc.sync.dma_start(
             out=w_codes[:, :, 0, :].bitcast(I32),
             in_=W_words.rearrange("j p t e -> p j (t e)").bitcast(I32),
@@ -55,21 +66,13 @@ def tile_neuralobliviousdecisiontree_e_kernel(tc, x, W_words, W_scales, b, leaf_
                 out=w_scales[32 * quadrant : 32 * quadrant + 4, :, 0, :].bitcast(I32),
                 in_=scale_rows[4 * quadrant : 4 * quadrant + 4, :, :],
             )
-        for q in range(1, N_CHUNKS):
-            nc.sync.dma_start(out=x_raw[q][:], in_=x_rows[:, q * CHUNK_TILES : (q + 1) * CHUNK_TILES, :])
-        nc.vector.tensor_copy(out=w_codes[:, :, 1, :].bitcast(I32), in_=w_codes[:, :, 0, :].bitcast(I32))
-        nc.vector.tensor_copy(out=w_scales[:, :, 1, :].bitcast(I32), in_=w_scales[:, :, 0, :].bitcast(I32))
-
-        b_rows = const.tile([P, P], BF16)
-        nc.vector.memset(b_rows[:], 0.0)
-        leaf_raw = const.tile([P, LEAVES // 2, D_OUT], BF16)
         for b0 in range(2):
-            nc.scalar.dma_start(out=b_rows[0:DEPTH, TREES * b0 : TREES * (b0 + 1)], in_=b)
-        for b0 in range(2):
-            nc.scalar.dma_start(
+            nc.sync.dma_start(
                 out=leaf_raw[TREES * b0 : TREES * (b0 + 1), :, :],
                 in_=leaf_values[:, (LEAVES // 2) * b0 : (LEAVES // 2) * (b0 + 1), :],
             )
+        load_x(2)
+        load_x(3)
 
         ident = const.tile([P, P], F32)
         make_identity(nc, ident[:])
@@ -89,25 +92,17 @@ def tile_neuralobliviousdecisiontree_e_kernel(tc, x, W_words, W_scales, b, leaf_
         nc.vector.tensor_copy(out=bias_keep[:], in_=b_cols[:, 0:DEPTH])
         nc.vector.tensor_scalar_mul(out=bias_flip[:], in0=b_cols[:, 0:DEPTH], scalar1=-1.0)
         nc.vector.tensor_tensor(out=half_bias[:], in0=bias_keep[:, 0:1], in1=half_sign[:], op=MULT)
+        nc.vector.tensor_copy(out=w_codes[:, :, 1, :].bitcast(I32), in_=w_codes[:, :, 0, :].bitcast(I32))
+        nc.vector.tensor_copy(out=w_scales[:, :, 1, :].bitcast(I32), in_=w_scales[:, :, 0, :].bitcast(I32))
 
-        leaf_grouped = const.tile([P, PASSES, D_OUT, PACK], BF16, align_bytes=64)
-        leaf_codes = const.tile([P, PASSES, D_OUT], U32, align_bytes=64)
-        leaf_scales = const.tile([P, PASSES, D_OUT], U8, align_bytes=64)
-        nc.vector.tensor_copy(out=leaf_grouped[:], in_=leaf_raw[:].rearrange("p (g j) d -> p g d j", j=PACK))
-        nc.vector.quantize_mx(
-            out=leaf_codes[:].rearrange("p g d -> p (g d)").bitcast(FP8X4),
-            scales=leaf_scales[:].rearrange("p g d -> p (g d)"),
-            in_=leaf_grouped[:].rearrange("p g d j -> p (g d j)"),
-        )
+        x_grouped = {}
+        x_mx = {}
 
-        upper = {}
-        lower = {}
-
-        def split_probabilities(q):
+        def transpose_x(q):
             x_words = x_raw[q][:].rearrange("p c f -> p (c f)").bitcast(F32)
             words_per_row = FEATURES // 2
-            x_grouped = x_pool.tile([P, CHUNK * PACK], BF16, align_bytes=64)
-            grouped_words = x_grouped[:].bitcast(F32).rearrange("p (c n u) -> p c n u", c=CHUNK_TILES, u=2)
+            grouped = x_pool.tile([P, CHUNK * PACK], BF16, align_bytes=64, name="x_grouped")
+            grouped_words = grouped[:].bitcast(F32).rearrange("p (c n u) -> p c n u", c=CHUNK_TILES, u=2)
             for pair in range(CHUNK_TILES // 2):
                 x_t = psum.tile([P, 2, 2, P], F32, tag="x_t")
                 for i in range(2):
@@ -122,12 +117,21 @@ def tile_neuralobliviousdecisiontree_e_kernel(tc, x, W_words, W_scales, b, leaf_
                     out=grouped_words[:, 2 * pair : 2 * pair + 2, :, :],
                     in_=x_t[:].rearrange("p c u n -> p c n u"),
                 )
+            x_grouped[q] = grouped
+
+        def quantise_x(q):
             x_codes = x_pool.tile([P, CHUNK], U32, align_bytes=64)
             x_scales = x_pool.tile([P, CHUNK], U8, align_bytes=64)
-            nc.vector.quantize_mx(out=x_codes[:].bitcast(FP8X4), scales=x_scales[:], in_=x_grouped[:])
+            nc.vector.quantize_mx(out=x_codes[:].bitcast(FP8X4), scales=x_scales[:], in_=x_grouped[q][:])
+            x_mx[q] = (x_codes, x_scales)
 
-            factors = []
-            for level in range(DEPTH):
+        upper = {}
+        lower = {}
+
+        def split_probabilities(q, eng):
+            x_codes, x_scales = x_mx[q]
+            factors = {}
+            for level in LEVEL_ORDER:
                 z = psum.tile([P, CHUNK], F32, tag="z")
                 nc.tensor.matmul_mx(
                     out=z[:],
@@ -149,54 +153,59 @@ def tile_neuralobliviousdecisiontree_e_kernel(tc, x, W_words, W_scales, b, leaf_
                     nc.scalar.activation(
                         out=f[:, 1, :], in_=z[:], func=SIGMOID, bias=bias_flip[:, level : level + 1], scale=-1.0
                     )
-                factors.append(f)
+                factors[level] = f
 
-            eng = nc.vector if q == 0 else nc.gpsimd
-            f0, f1, f2, f3, f4, f5 = factors
             c4 = factor_pool.tile([P, CHUNK, 2, 2], F32, name="c4")
             eng.tensor_tensor(
                 out=c4[:],
-                in0=f4[:].rearrange("p b n -> p n b").unsqueeze(3).to_broadcast([P, CHUNK, 2, 2]),
-                in1=f5[:].rearrange("p b n -> p n b").unsqueeze(2).to_broadcast([P, CHUNK, 2, 2]),
+                in0=factors[4][:].rearrange("p b n -> p n b").unsqueeze(3).to_broadcast([P, CHUNK, 2, 2]),
+                in1=factors[5][:].rearrange("p b n -> p n b").unsqueeze(2).to_broadcast([P, CHUNK, 2, 2]),
                 op=MULT,
             )
             a2 = factor_pool.tile([P, 2, CHUNK], F32, name="a2")
-            eng.tensor_tensor(out=a2[:], in0=f0[:].unsqueeze(1).to_broadcast([P, 2, CHUNK]), in1=f1[:], op=MULT)
+            eng.tensor_tensor(
+                out=a2[:], in0=factors[0][:].unsqueeze(1).to_broadcast([P, 2, CHUNK]), in1=factors[1][:], op=MULT
+            )
             a4 = factor_pool.tile([P, 2, 2, CHUNK], F32, name="a4")
             eng.tensor_tensor(
                 out=a4[:],
                 in0=a2[:].unsqueeze(2).to_broadcast([P, 2, 2, CHUNK]),
-                in1=f2[:].unsqueeze(1).to_broadcast([P, 2, 2, CHUNK]),
+                in1=factors[2][:].unsqueeze(1).to_broadcast([P, 2, 2, CHUNK]),
                 op=MULT,
             )
             a8 = factor_pool.tile([P, 4, 2, CHUNK], F32, name="a8")
             eng.tensor_tensor(
                 out=a8[:],
                 in0=a4[:].rearrange("p a b n -> p (a b) n").unsqueeze(2).to_broadcast([P, 4, 2, CHUNK]),
-                in1=f3[:].unsqueeze(1).to_broadcast([P, 4, 2, CHUNK]),
+                in1=factors[3][:].unsqueeze(1).to_broadcast([P, 4, 2, CHUNK]),
                 op=MULT,
             )
             upper[q] = a8[:].rearrange("p a b n -> p (a b) n")
             lower[q] = c4[:].rearrange("p n a b -> p n (a b)")
 
+        lower_banks = {}
+
+        def copy_lower(t):
+            q, i = divmod(t, CHUNK_TILES)
+            lower_ps = psum.tile([P, P, PACK], F32, tag="lower_ps", bufs=3)
+            nc.tensor.matmul(
+                out=lower_ps[:].rearrange("p n j -> p (n j)"),
+                lhsT=ident[:],
+                rhs=lower[q][:, i * P : (i + 1) * P, :].rearrange("p n j -> p (n j)"),
+                start=True,
+                stop=True,
+            )
+            lower_banks[t] = lower_ps
+
         paths = {}
 
         def multiply(t):
             q, i = divmod(t, CHUNK_TILES)
-            columns = slice(i * P, (i + 1) * P)
-            lower_ps = psum.tile([P, P, PACK], F32, tag="lower_ps")
-            nc.tensor.matmul(
-                out=lower_ps[:].rearrange("p n j -> p (n j)"),
-                lhsT=ident[:],
-                rhs=lower[q][:, columns, :].rearrange("p n j -> p (n j)"),
-                start=True,
-                stop=True,
-            )
             path = path_pool.tile([P, PASSES, P, PACK], BF16, align_bytes=64)
             nc.vector.tensor_tensor(
                 out=path[:],
-                in0=upper[q][:, :, columns].unsqueeze(3).to_broadcast([P, PASSES, P, PACK]),
-                in1=lower_ps[:].unsqueeze(1).to_broadcast([P, PASSES, P, PACK]),
+                in0=upper[q][:, :, i * P : (i + 1) * P].unsqueeze(3).to_broadcast([P, PASSES, P, PACK]),
+                in1=lower_banks[t][:].unsqueeze(1).to_broadcast([P, PASSES, P, PACK]),
                 op=MULT,
             )
             paths[t] = path
@@ -212,7 +221,7 @@ def tile_neuralobliviousdecisiontree_e_kernel(tc, x, W_words, W_scales, b, leaf_
                 scales=path_scales[:].rearrange("p g n -> p (g n)"),
                 in_=paths[t][:].rearrange("p g n j -> p (g n j)"),
             )
-            acc = psum.tile([P, D_OUT], F32, tag="acc")
+            acc = psum.tile([P, D_OUT], F32, tag="acc", bufs=1)
             for g in range(PASSES):
                 nc.tensor.matmul_mx(
                     out=acc[:],
@@ -229,12 +238,37 @@ def tile_neuralobliviousdecisiontree_e_kernel(tc, x, W_words, W_scales, b, leaf_
             if i == CHUNK_TILES - 1:
                 nc.sync.dma_start(out=out_rows[:, q * CHUNK_TILES : (q + 1) * CHUNK_TILES, :], in_=results[q][:])
 
-        split_probabilities(0)
+        transpose_x(0)
+        quantise_x(0)
+        transpose_x(1)
+        quantise_x(1)
+
+        leaf_grouped = const.tile([P, PASSES, D_OUT, PACK], BF16, align_bytes=64)
+        leaf_codes = const.tile([P, PASSES, D_OUT], U32, align_bytes=64)
+        leaf_scales = const.tile([P, PASSES, D_OUT], U8, align_bytes=64)
+        nc.vector.tensor_copy(out=leaf_grouped[:], in_=leaf_raw[:].rearrange("p (g j) d -> p g d j", j=PACK))
+        nc.vector.quantize_mx(
+            out=leaf_codes[:].rearrange("p g d -> p (g d)").bitcast(FP8X4),
+            scales=leaf_scales[:].rearrange("p g d -> p (g d)"),
+            in_=leaf_grouped[:].rearrange("p g d j -> p (g d j)"),
+        )
+
+        split_probabilities(0, nc.vector)
+        copy_lower(0)
+        split_probabilities(1, nc.gpsimd)
+        copy_lower(1)
+        transpose_x(2)
+
         for t in range(N_TILES):
             q, i = divmod(t, CHUNK_TILES)
-            if i == 0 and q + 1 < N_CHUNKS:
-                split_probabilities(q + 1)
+            if t + 2 < N_TILES:
+                copy_lower(t + 2)
             multiply(t)
             if t >= 1:
                 contract(t - 1)
+            if i == 0 and q + 2 < N_CHUNKS:
+                quantise_x(q + 2)
+                split_probabilities(q + 2, nc.gpsimd)
+            if i == 1 and q + 3 < N_CHUNKS:
+                transpose_x(q + 3)
         contract(N_TILES - 1)

@@ -22,6 +22,7 @@ CHUNK_TILES = 4
 CHUNK = CHUNK_TILES * P
 N_CHUNKS = N_TILES // CHUNK_TILES
 LEVEL_ORDER = (4, 5, 0, 1, 2, 3)
+HALF_LEVELS = (0, 4)
 
 FLOPS = 2 * BATCH * FEATURES * DEPTH * TREES + 2 * BATCH * TREES * LEAVES * D_OUT
 
@@ -33,7 +34,7 @@ def tile_neuralobliviousdecisiontree_e_kernel(tc, x, W_words, W_scales, b, leaf_
         const = ctx.enter_context(tc.tile_pool(name="const", bufs=1))
         x_pool = ctx.enter_context(tc.tile_pool(name="x_pool", bufs=2))
         factor_pool = ctx.enter_context(tc.tile_pool(name="factor_pool", bufs=2))
-        path_pool = ctx.enter_context(tc.tile_pool(name="path_pool", bufs=3))
+        path_pool = ctx.enter_context(tc.tile_pool(name="path_pool", bufs=CHUNK_TILES))
         out_pool = ctx.enter_context(tc.tile_pool(name="out_pool", bufs=2))
         psum = ctx.enter_context(tc.psum_pool(name="psum", bufs=2))
 
@@ -88,10 +89,17 @@ def tile_neuralobliviousdecisiontree_e_kernel(tc, x, W_words, W_scales, b, leaf_
         nc.tensor.transpose(out=b_cols[:], in_=b_rows_f32[:], identity=ident[:])
         bias_keep = const.tile([P, DEPTH], F32)
         bias_flip = const.tile([P, DEPTH], F32)
-        half_bias = const.tile([P, 1], F32)
+        half_bias = const.tile([P, DEPTH], F32)
         nc.vector.tensor_copy(out=bias_keep[:], in_=b_cols[:, 0:DEPTH])
         nc.vector.tensor_scalar_mul(out=bias_flip[:], in0=b_cols[:, 0:DEPTH], scalar1=-1.0)
-        nc.vector.tensor_tensor(out=half_bias[:], in0=bias_keep[:, 0:1], in1=half_sign[:], op=MULT)
+        nc.vector.tensor_scalar_mul(out=half_bias[:], in0=b_cols[:, 0:DEPTH], scalar1=half_sign[:, 0:1])
+        select = []
+        for h in range(2):
+            select.append(const.tile([P, 2, TREES], F32, name="select%d" % h))
+            nc.vector.tensor_copy(
+                out=select[h][:],
+                in_=ident[:, TREES * h : TREES * (h + 1)].unsqueeze(1).to_broadcast([P, 2, TREES]),
+            )
         nc.vector.tensor_copy(out=w_codes[:, :, 1, :].bitcast(I32), in_=w_codes[:, :, 0, :].bitcast(I32))
         nc.vector.tensor_copy(out=w_scales[:, :, 1, :].bitcast(I32), in_=w_scales[:, :, 0, :].bitcast(I32))
 
@@ -120,8 +128,8 @@ def tile_neuralobliviousdecisiontree_e_kernel(tc, x, W_words, W_scales, b, leaf_
             x_grouped[q] = grouped
 
         def quantise_x(q):
-            x_codes = x_pool.tile([P, CHUNK], U32, align_bytes=64)
-            x_scales = x_pool.tile([P, CHUNK], U8, align_bytes=64)
+            x_codes = const.tile([P, CHUNK], U32, align_bytes=64, name="x_codes%d" % q)
+            x_scales = const.tile([P, CHUNK], U8, align_bytes=64, name="x_scales%d" % q)
             nc.vector.quantize_mx(out=x_codes[:].bitcast(FP8X4), scales=x_scales[:], in_=x_grouped[q][:])
             x_mx[q] = (x_codes, x_scales)
 
@@ -142,9 +150,11 @@ def tile_neuralobliviousdecisiontree_e_kernel(tc, x, W_words, W_scales, b, leaf_
                     start=True,
                     stop=True,
                 )
-                if level == 0:
-                    f = factor_pool.tile([P, CHUNK], F32, name="f0")
-                    nc.scalar.activation(out=f[:], in_=z[:], func=SIGMOID, bias=half_bias[:], scale=half_sign[:])
+                if level in HALF_LEVELS:
+                    f = factor_pool.tile([P, CHUNK], F32, name="f%d" % level)
+                    nc.scalar.activation(
+                        out=f[:], in_=z[:], func=SIGMOID, bias=half_bias[:, level : level + 1], scale=half_sign[:]
+                    )
                 else:
                     f = factor_pool.tile([P, 2, CHUNK], F32, name="f%d" % level)
                     nc.scalar.activation(
@@ -155,12 +165,9 @@ def tile_neuralobliviousdecisiontree_e_kernel(tc, x, W_words, W_scales, b, leaf_
                     )
                 factors[level] = f
 
-            c4 = factor_pool.tile([P, CHUNK, 2, 2], F32, name="c4")
+            c2 = factor_pool.tile([P, 2, CHUNK], F32, name="c2")
             eng.tensor_tensor(
-                out=c4[:],
-                in0=factors[4][:].rearrange("p b n -> p n b").unsqueeze(3).to_broadcast([P, CHUNK, 2, 2]),
-                in1=factors[5][:].rearrange("p b n -> p n b").unsqueeze(2).to_broadcast([P, CHUNK, 2, 2]),
-                op=MULT,
+                out=c2[:], in0=factors[4][:].unsqueeze(1).to_broadcast([P, 2, CHUNK]), in1=factors[5][:], op=MULT
             )
             a2 = factor_pool.tile([P, 2, CHUNK], F32, name="a2")
             eng.tensor_tensor(
@@ -181,20 +188,22 @@ def tile_neuralobliviousdecisiontree_e_kernel(tc, x, W_words, W_scales, b, leaf_
                 op=MULT,
             )
             upper[q] = a8[:].rearrange("p a b n -> p (a b) n")
-            lower[q] = c4[:].rearrange("p n a b -> p n (a b)")
+            lower[q] = c2
 
         lower_banks = {}
 
         def copy_lower(t):
             q, i = divmod(t, CHUNK_TILES)
             lower_ps = psum.tile([P, P, PACK], F32, tag="lower_ps", bufs=3)
-            nc.tensor.matmul(
-                out=lower_ps[:].rearrange("p n j -> p (n j)"),
-                lhsT=ident[:],
-                rhs=lower[q][:, i * P : (i + 1) * P, :].rearrange("p n j -> p (n j)"),
-                start=True,
-                stop=True,
-            )
+            for b4 in range(2):
+                for b5 in range(2):
+                    nc.tensor.matmul(
+                        out=lower_ps[:, :, 2 * b4 + b5],
+                        lhsT=select[b4][:].rearrange("p h t -> p (h t)"),
+                        rhs=lower[q][:, b5, i * P : (i + 1) * P],
+                        start=True,
+                        stop=True,
+                    )
             lower_banks[t] = lower_ps
 
         paths = {}
@@ -254,21 +263,21 @@ def tile_neuralobliviousdecisiontree_e_kernel(tc, x, W_words, W_scales, b, leaf_
         )
 
         split_probabilities(0, nc.vector)
-        copy_lower(0)
-        split_probabilities(1, nc.gpsimd)
-        copy_lower(1)
         transpose_x(2)
+        quantise_x(2)
+        transpose_x(3)
+        quantise_x(3)
+        copy_lower(0)
+        copy_lower(1)
+        split_probabilities(1, nc.gpsimd)
 
-        for t in range(N_TILES):
-            q, i = divmod(t, CHUNK_TILES)
-            if t + 2 < N_TILES:
-                copy_lower(t + 2)
-            multiply(t)
-            if t >= 1:
-                contract(t - 1)
-            if i == 0 and q + 2 < N_CHUNKS:
-                quantise_x(q + 2)
-                split_probabilities(q + 2, nc.gpsimd)
-            if i == 1 and q + 3 < N_CHUNKS:
-                transpose_x(q + 3)
-        contract(N_TILES - 1)
+        for q in range(N_CHUNKS):
+            for i in range(CHUNK_TILES):
+                t = q * CHUNK_TILES + i
+                if t + 2 < N_TILES:
+                    copy_lower(t + 2)
+                multiply(t)
+                if i == 1 and q + 2 < N_CHUNKS:
+                    split_probabilities(q + 2, nc.gpsimd)
+            for i in range(CHUNK_TILES):
+                contract(q * CHUNK_TILES + i)

@@ -85,14 +85,6 @@ def tile_neuralobliviousdecisiontree_e_kernel(tc, x, W_words, W_scales, b, leaf_
 
         b_rows_f32 = const.tile([P, P], F32)
         nc.vector.tensor_copy(out=b_rows_f32[:], in_=b_rows[:])
-        b_cols = psum.tile([P, P], F32, tag="x_t")
-        nc.tensor.transpose(out=b_cols[:], in_=b_rows_f32[:], identity=ident[:])
-        bias_keep = const.tile([P, DEPTH], F32)
-        bias_flip = const.tile([P, DEPTH], F32)
-        half_bias = const.tile([P, DEPTH], F32)
-        nc.vector.tensor_copy(out=bias_keep[:], in_=b_cols[:, 0:DEPTH])
-        nc.vector.tensor_scalar_mul(out=bias_flip[:], in0=b_cols[:, 0:DEPTH], scalar1=-1.0)
-        nc.vector.tensor_scalar_mul(out=half_bias[:], in0=b_cols[:, 0:DEPTH], scalar1=half_sign[:, 0:1])
         select = []
         for h in range(2):
             select.append(const.tile([P, 2, TREES], F32, name="select%d" % h))
@@ -102,6 +94,20 @@ def tile_neuralobliviousdecisiontree_e_kernel(tc, x, W_words, W_scales, b, leaf_
             )
         nc.vector.tensor_copy(out=w_codes[:, :, 1, :].bitcast(I32), in_=w_codes[:, :, 0, :].bitcast(I32))
         nc.vector.tensor_copy(out=w_scales[:, :, 1, :].bitcast(I32), in_=w_scales[:, :, 0, :].bitcast(I32))
+
+        leaf_grouped = const.tile([P, PASSES, D_OUT, PACK], BF16, align_bytes=64)
+        leaf_codes = const.tile([P, PASSES, D_OUT], U32, align_bytes=64)
+        leaf_scales = const.tile([P, PASSES, D_OUT], U8, align_bytes=64)
+
+        def regroup_leaves():
+            nc.scalar.copy(out=leaf_grouped[:], in_=leaf_raw[:].rearrange("p (g j) d -> p g d j", j=PACK))
+
+        def quantise_leaves():
+            nc.vector.quantize_mx(
+                out=leaf_codes[:].rearrange("p g d -> p (g d)").bitcast(FP8X4),
+                scales=leaf_scales[:].rearrange("p g d -> p (g d)"),
+                in_=leaf_grouped[:].rearrange("p g d j -> p (g d j)"),
+            )
 
         x_grouped = {}
         x_mx = {}
@@ -208,10 +214,15 @@ def tile_neuralobliviousdecisiontree_e_kernel(tc, x, W_words, W_scales, b, leaf_
 
         paths = {}
 
-        def multiply(t):
+        def lower_to_sbuf(t):
+            lower_sb = const.tile([P, P, PACK], F32)
+            nc.scalar.copy(out=lower_sb[:], in_=lower_banks[t][:])
+            lower_banks[t] = lower_sb
+
+        def multiply(t, eng):
             q, i = divmod(t, CHUNK_TILES)
             path = path_pool.tile([P, PASSES, P, PACK], BF16, align_bytes=64)
-            nc.vector.tensor_tensor(
+            eng.tensor_tensor(
                 out=path[:],
                 in0=upper[q][:, :, i * P : (i + 1) * P].unsqueeze(3).to_broadcast([P, PASSES, P, PACK]),
                 in1=lower_banks[t][:].unsqueeze(1).to_broadcast([P, PASSES, P, PACK]),
@@ -248,19 +259,17 @@ def tile_neuralobliviousdecisiontree_e_kernel(tc, x, W_words, W_scales, b, leaf_
                 nc.sync.dma_start(out=out_rows[:, q * CHUNK_TILES : (q + 1) * CHUNK_TILES, :], in_=results[q][:])
 
         transpose_x(0)
+        b_cols = psum.tile([P, P], F32, tag="x_t")
+        nc.tensor.transpose(out=b_cols[:], in_=b_rows_f32[:], identity=ident[:])
+        bias_keep = const.tile([P, DEPTH], F32)
+        bias_flip = const.tile([P, DEPTH], F32)
+        half_bias = const.tile([P, DEPTH], F32)
+        nc.vector.tensor_copy(out=bias_keep[:], in_=b_cols[:, 0:DEPTH])
+        nc.vector.tensor_scalar_mul(out=bias_flip[:], in0=b_cols[:, 0:DEPTH], scalar1=-1.0)
+        nc.vector.tensor_scalar_mul(out=half_bias[:], in0=b_cols[:, 0:DEPTH], scalar1=half_sign[:, 0:1])
         quantise_x(0)
         transpose_x(1)
         quantise_x(1)
-
-        leaf_grouped = const.tile([P, PASSES, D_OUT, PACK], BF16, align_bytes=64)
-        leaf_codes = const.tile([P, PASSES, D_OUT], U32, align_bytes=64)
-        leaf_scales = const.tile([P, PASSES, D_OUT], U8, align_bytes=64)
-        nc.vector.tensor_copy(out=leaf_grouped[:], in_=leaf_raw[:].rearrange("p (g j) d -> p g d j", j=PACK))
-        nc.vector.quantize_mx(
-            out=leaf_codes[:].rearrange("p g d -> p (g d)").bitcast(FP8X4),
-            scales=leaf_scales[:].rearrange("p g d -> p (g d)"),
-            in_=leaf_grouped[:].rearrange("p g d j -> p (g d j)"),
-        )
 
         split_probabilities(0, nc.vector)
         transpose_x(2)
@@ -270,14 +279,21 @@ def tile_neuralobliviousdecisiontree_e_kernel(tc, x, W_words, W_scales, b, leaf_
         copy_lower(0)
         copy_lower(1)
         split_probabilities(1, nc.gpsimd)
+        regroup_leaves()
 
         for q in range(N_CHUNKS):
             for i in range(CHUNK_TILES):
                 t = q * CHUNK_TILES + i
                 if t + 2 < N_TILES:
                     copy_lower(t + 2)
-                multiply(t)
+                if q == N_CHUNKS - 1 and i == 0:
+                    lower_to_sbuf(t)
+                    multiply(t, nc.gpsimd)
+                else:
+                    multiply(t, nc.vector)
                 if i == 1 and q + 2 < N_CHUNKS:
                     split_probabilities(q + 2, nc.gpsimd)
+            if q == 0:
+                quantise_leaves()
             for i in range(CHUNK_TILES):
                 contract(q * CHUNK_TILES + i)

@@ -11,8 +11,11 @@ U8 = mybir.dt.uint8
 FP8X4 = mybir.dt.float8_e4m3fn_x4
 MULT = mybir.AluOpType.mult
 SIGMOID = mybir.ActivationFunctionType.Sigmoid
+LN = mybir.ActivationFunctionType.Ln
+EXP = mybir.ActivationFunctionType.Exp
 COPY = mybir.ActivationFunctionType.Copy
 
+PINNED = {mybir.EngineType.Activation, mybir.EngineType.DVE, mybir.EngineType.Pool, mybir.EngineType.SP}
 P = 128
 PACK = 4
 BATCH, FEATURES, DEPTH, TREES, LEAVES, D_OUT = 2048, 512, 6, 64, 64, 128
@@ -21,8 +24,10 @@ N_TILES = BATCH // P
 CHUNK_TILES = 4
 CHUNK = CHUNK_TILES * P
 N_CHUNKS = N_TILES // CHUNK_TILES
+N_PRODUCT = 12
 LEVEL_ORDER = (4, 5, 0, 1, 2, 3)
 HALF_LEVELS = (0, 4)
+LOG_PATHS = 4
 
 FLOPS = 2 * BATCH * FEATURES * DEPTH * TREES + 2 * BATCH * TREES * LEAVES * D_OUT
 
@@ -30,11 +35,13 @@ FLOPS = 2 * BATCH * FEATURES * DEPTH * TREES + 2 * BATCH * TREES * LEAVES * D_OU
 def tile_neuralobliviousdecisiontree_e_kernel(tc, x, W_words, W_scales, b, leaf_values, out):
     nc = tc.nc
     with ExitStack() as ctx:
-        ctx.enter_context(tc.manual_schedule())
+        ctx.enter_context(tc.manual_schedule(engines=PINNED))
         const = ctx.enter_context(tc.tile_pool(name="const", bufs=1))
-        x_pool = ctx.enter_context(tc.tile_pool(name="x_pool", bufs=2))
+        x_pool = ctx.enter_context(tc.tile_pool(name="x_pool", bufs=3))
         factor_pool = ctx.enter_context(tc.tile_pool(name="factor_pool", bufs=2))
-        path_pool = ctx.enter_context(tc.tile_pool(name="path_pool", bufs=CHUNK_TILES))
+        scratch_pool = ctx.enter_context(tc.tile_pool(name="scratch_pool", bufs=4))
+        product_pool = ctx.enter_context(tc.tile_pool(name="product_pool", bufs=3))
+        path_pool = ctx.enter_context(tc.tile_pool(name="path_pool", bufs=4))
         out_pool = ctx.enter_context(tc.tile_pool(name="out_pool", bufs=2))
         psum = ctx.enter_context(tc.psum_pool(name="psum", bufs=2))
 
@@ -42,21 +49,23 @@ def tile_neuralobliviousdecisiontree_e_kernel(tc, x, W_words, W_scales, b, leaf_
         out_rows = out.rearrange("(p c) d -> p c d", c=N_TILES)
         x_raw = []
         for q in range(N_CHUNKS):
-            x_raw.append(const.tile([P, CHUNK_TILES, FEATURES], BF16, name="x_raw%d" % q))
+            x_raw.append(scratch_pool.tile([P, CHUNK_TILES, FEATURES], BF16, tag="scratch", name="x_raw"))
 
-        def load_x(q):
-            nc.sync.dma_start(out=x_raw[q][:], in_=x_rows[:, q * CHUNK_TILES : (q + 1) * CHUNK_TILES, :])
+        def load_x(q, lo, hi):
+            nc.sync.dma_start(
+                out=x_raw[q][:, lo:hi, :], in_=x_rows[:, q * CHUNK_TILES + lo : q * CHUNK_TILES + hi, :]
+            )
 
         w_codes = const.tile([P, DEPTH, 2, TREES], U32, align_bytes=64)
         w_scales = const.tile([P, DEPTH, 2, TREES], U8, align_bytes=64)
         b_rows = const.tile([P, P], BF16)
-        leaf_raw = const.tile([P, LEAVES // 2, D_OUT], BF16)
+        leaf_raw = path_pool.tile([P, LEAVES // 2, D_OUT], BF16, align_bytes=64, tag="log_path", bufs=LOG_PATHS, name="leaf_raw")
         nc.vector.memset(w_scales[:].rearrange("p j h t -> p (j h t)").bitcast(I32), 0)
         nc.vector.memset(b_rows[:], 0.0)
         for b0 in range(2):
             nc.scalar.dma_start(out=b_rows[0:DEPTH, TREES * b0 : TREES * (b0 + 1)], in_=b)
-        load_x(0)
-        load_x(1)
+        load_x(0, 0, 2)
+        load_x(0, 2, 4)
         nc.sync.dma_start(
             out=w_codes[:, :, 0, :].bitcast(I32),
             in_=W_words.rearrange("j p t e -> p j (t e)").bitcast(I32),
@@ -67,40 +76,44 @@ def tile_neuralobliviousdecisiontree_e_kernel(tc, x, W_words, W_scales, b, leaf_
                 out=w_scales[32 * quadrant : 32 * quadrant + 4, :, 0, :].bitcast(I32),
                 in_=scale_rows[4 * quadrant : 4 * quadrant + 4, :, :],
             )
-        for b0 in range(2):
-            nc.sync.dma_start(
-                out=leaf_raw[TREES * b0 : TREES * (b0 + 1), :, :],
-                in_=leaf_values[:, (LEAVES // 2) * b0 : (LEAVES // 2) * (b0 + 1), :],
-            )
-        load_x(2)
-        load_x(3)
+        load_x(1, 0, 4)
+        half_leaves = LEAVES // 2
+        nc.sync.dma_start(out=leaf_raw[0:TREES, :, :], in_=leaf_values[:, 0:half_leaves, :])
+        load_x(2, 0, 4)
+        load_x(3, 0, 4)
+        for k in range(half_leaves):
+            nc.sync.dma_start(out=leaf_raw[TREES:P, k, :], in_=leaf_values[:, LEAVES - 1 - k, :])
 
         ident = const.tile([P, P], F32)
         make_identity(nc, ident[:])
-        half_sign = const.tile([P, 1], F32)
-        nc.vector.memset(half_sign[0:TREES, :], 1.0)
-        nc.vector.memset(half_sign[TREES:P, :], -1.0)
+        half_sign = const.tile([P, 2], F32)
+        nc.vector.memset(half_sign[:], -1.0)
+        nc.vector.memset(half_sign[0:TREES, 0:1], 1.0)
+        nc.vector.memset(half_sign[TREES:P, 1:2], 1.0)
+        floor = const.tile([P, 1], F32)
+        nc.vector.memset(floor[:], 1e-30)
         table_warmer = const.tile([P, 1], F32)
-        nc.scalar.activation(out=table_warmer[:], in_=half_sign[:], func=SIGMOID)
+        nc.scalar.activation(out=table_warmer[:], in_=half_sign[:, 0:1], func=SIGMOID)
 
         b_rows_f32 = const.tile([P, P], F32)
         nc.vector.tensor_copy(out=b_rows_f32[:], in_=b_rows[:])
-        select = []
-        for h in range(2):
-            select.append(const.tile([P, 2, TREES], F32, name="select%d" % h))
-            nc.vector.tensor_copy(
-                out=select[h][:],
-                in_=ident[:, TREES * h : TREES * (h + 1)].unsqueeze(1).to_broadcast([P, 2, TREES]),
-            )
+        swap = const.tile([P, P], F32)
+        nc.vector.tensor_copy(out=swap[:, 0:TREES], in_=ident[:, TREES:P])
+        nc.vector.tensor_copy(out=swap[:, TREES:P], in_=ident[:, 0:TREES])
         nc.vector.tensor_copy(out=w_codes[:, :, 1, :].bitcast(I32), in_=w_codes[:, :, 0, :].bitcast(I32))
         nc.vector.tensor_copy(out=w_scales[:, :, 1, :].bitcast(I32), in_=w_scales[:, :, 0, :].bitcast(I32))
 
-        leaf_grouped = const.tile([P, PASSES, D_OUT, PACK], BF16, align_bytes=64)
+        leaf_grouped = path_pool.tile(
+            [P, PASSES, D_OUT, PACK], BF16, align_bytes=64, tag="log_path", bufs=LOG_PATHS, name="leaf_grouped"
+        )
         leaf_codes = const.tile([P, PASSES, D_OUT], U32, align_bytes=64)
         leaf_scales = const.tile([P, PASSES, D_OUT], U8, align_bytes=64)
 
-        def regroup_leaves():
-            nc.scalar.copy(out=leaf_grouped[:], in_=leaf_raw[:].rearrange("p (g j) d -> p g d j", j=PACK))
+        def regroup_leaves(lo, hi):
+            nc.vector.tensor_copy(
+                out=leaf_grouped[:, lo:hi, :, :],
+                in_=leaf_raw[:, PACK * lo : PACK * hi, :].rearrange("p (g j) d -> p g d j", j=PACK),
+            )
 
         def quantise_leaves():
             nc.vector.quantize_mx(
@@ -112,26 +125,25 @@ def tile_neuralobliviousdecisiontree_e_kernel(tc, x, W_words, W_scales, b, leaf_
         x_grouped = {}
         x_mx = {}
 
-        def transpose_x(q):
+        def transpose_x(q, pair, eng_copy):
             x_words = x_raw[q][:].rearrange("p c f -> p (c f)").bitcast(F32)
             words_per_row = FEATURES // 2
-            grouped = x_pool.tile([P, CHUNK * PACK], BF16, align_bytes=64, name="x_grouped")
-            grouped_words = grouped[:].bitcast(F32).rearrange("p (c n u) -> p c n u", c=CHUNK_TILES, u=2)
-            for pair in range(CHUNK_TILES // 2):
-                x_t = psum.tile([P, 2, 2, P], F32, tag="x_t")
-                for i in range(2):
-                    first = (2 * pair + i) * words_per_row
-                    for u in range(2):
-                        nc.tensor.transpose(
-                            out=x_t[:, i, u, :],
-                            in_=x_words[:, first + u : first + words_per_row : 2],
-                            identity=ident[:],
-                        )
-                nc.scalar.copy(
-                    out=grouped_words[:, 2 * pair : 2 * pair + 2, :, :],
-                    in_=x_t[:].rearrange("p c u n -> p c n u"),
-                )
-            x_grouped[q] = grouped
+            if pair == 0:
+                x_grouped[q] = x_pool.tile([P, CHUNK * PACK], BF16, align_bytes=64, name="x_grouped")
+            grouped_words = x_grouped[q][:].bitcast(F32).rearrange("p (c n u) -> p c n u", c=CHUNK_TILES, u=2)
+            x_t = psum.tile([P, 2, 2, P], F32, tag="x_t")
+            for i in range(2):
+                first = (2 * pair + i) * words_per_row
+                for u in range(2):
+                    nc.tensor.transpose(
+                        out=x_t[:, i, u, :],
+                        in_=x_words[:, first + u : first + words_per_row : 2],
+                        identity=ident[:],
+                    )
+            eng_copy(
+                out=grouped_words[:, 2 * pair : 2 * pair + 2, :, :],
+                in_=x_t[:].rearrange("p c u n -> p c n u"),
+            )
 
         def quantise_x(q):
             x_codes = const.tile([P, CHUNK], U32, align_bytes=64, name="x_codes%d" % q)
@@ -139,112 +151,202 @@ def tile_neuralobliviousdecisiontree_e_kernel(tc, x, W_words, W_scales, b, leaf_
             nc.vector.quantize_mx(out=x_codes[:].bitcast(FP8X4), scales=x_scales[:], in_=x_grouped[q][:])
             x_mx[q] = (x_codes, x_scales)
 
+        def logits(level, first, n):
+            q, i = divmod(first, CHUNK_TILES)
+            cols = slice(i * P, (i + n) * P)
+            x_codes, x_scales = x_mx[q]
+            z = psum.tile([P, CHUNK], F32, tag="z")
+            nc.tensor.matmul_mx(
+                out=z[:, 0 : n * P],
+                lhsT=w_codes[:, level, :, :].rearrange("p h t -> p (h t)").bitcast(FP8X4),
+                lhsT_scale=w_scales[:, level, :, :].rearrange("p h t -> p (h t)"),
+                rhs=x_codes[:, cols].bitcast(FP8X4),
+                rhs_scale=x_scales[:, cols],
+                start=True,
+                stop=True,
+            )
+            return z[:, 0 : n * P]
+
+        def factor(out_ap, z, level, s):
+            nc.scalar.activation(
+                out=out_ap, in_=z, func=SIGMOID, bias=half_bias[:, s, level : level + 1], scale=half_sign[:, s : s + 1]
+            )
+
+        factors = {}
+
+        def factor_steps(first, n):
+            q, i = divmod(first, CHUNK_TILES)
+            cols = slice(i * P, (i + n) * P)
+            steps = []
+            for level in LEVEL_ORDER:
+
+                def step_0(level=level):
+                    half = level in HALF_LEVELS
+                    if (q, level) not in factors:
+                        factors[(q, level)] = factor_pool.tile([P, 1 if half else 2, CHUNK], F32, name="f%d" % level)
+                    zs[0] = logits(level, first, n)
+                    factor(factors[(q, level)][:, 0, cols], zs[0], level, 0)
+
+                def step_1(level=level):
+                    factor(factors[(q, level)][:, 1, cols], zs[0], level, 1)
+
+                steps.append(step_0)
+                if level not in HALF_LEVELS:
+                    steps.append(step_1)
+            return steps
+
         upper = {}
         lower = {}
 
-        def split_probabilities(q, eng):
-            x_codes, x_scales = x_mx[q]
-            factors = {}
-            for level in LEVEL_ORDER:
-                z = psum.tile([P, CHUNK], F32, tag="z")
-                nc.tensor.matmul_mx(
-                    out=z[:],
-                    lhsT=w_codes[:, level, :, :].rearrange("p h t -> p (h t)").bitcast(FP8X4),
-                    lhsT_scale=w_scales[:, level, :, :].rearrange("p h t -> p (h t)"),
-                    rhs=x_codes[:].bitcast(FP8X4),
-                    rhs_scale=x_scales[:],
-                    start=True,
-                    stop=True,
-                )
-                if level in HALF_LEVELS:
-                    f = factor_pool.tile([P, CHUNK], F32, name="f%d" % level)
-                    nc.scalar.activation(
-                        out=f[:], in_=z[:], func=SIGMOID, bias=half_bias[:, level : level + 1], scale=half_sign[:]
-                    )
-                else:
-                    f = factor_pool.tile([P, 2, CHUNK], F32, name="f%d" % level)
-                    nc.scalar.activation(
-                        out=f[:, 0, :], in_=z[:], func=SIGMOID, bias=bias_keep[:, level : level + 1], scale=1.0
-                    )
-                    nc.scalar.activation(
-                        out=f[:, 1, :], in_=z[:], func=SIGMOID, bias=bias_flip[:, level : level + 1], scale=-1.0
-                    )
-                factors[level] = f
-
-            c2 = factor_pool.tile([P, 2, CHUNK], F32, name="c2")
-            eng.tensor_tensor(
-                out=c2[:], in0=factors[4][:].unsqueeze(1).to_broadcast([P, 2, CHUNK]), in1=factors[5][:], op=MULT
-            )
-            a2 = factor_pool.tile([P, 2, CHUNK], F32, name="a2")
-            eng.tensor_tensor(
-                out=a2[:], in0=factors[0][:].unsqueeze(1).to_broadcast([P, 2, CHUNK]), in1=factors[1][:], op=MULT
-            )
-            a4 = factor_pool.tile([P, 2, 2, CHUNK], F32, name="a4")
+        def prepare(t, n, eng):
+            q, i = divmod(t, CHUNK_TILES)
+            cols = slice(i * P, (i + n) * P)
+            f = []
+            for level in range(DEPTH):
+                f.append(factors[(q, level)][:, :, cols])
+            w = n * P
+            c2 = product_pool.tile([P, 2, w], F32, name="c2_%d" % n, bufs=4 - n)
+            eng.tensor_tensor(out=c2[:], in0=f[4].to_broadcast([P, 2, w]), in1=f[5], op=MULT)
+            a2 = product_pool.tile([P, 2, w], F32, name="a2_%d" % n, bufs=1)
+            eng.tensor_tensor(out=a2[:], in0=f[0].to_broadcast([P, 2, w]), in1=f[1], op=MULT)
+            a4 = product_pool.tile([P, 2, 2, w], F32, name="a4_%d" % n, bufs=1)
             eng.tensor_tensor(
                 out=a4[:],
-                in0=a2[:].unsqueeze(2).to_broadcast([P, 2, 2, CHUNK]),
-                in1=factors[2][:].unsqueeze(1).to_broadcast([P, 2, 2, CHUNK]),
+                in0=a2[:].unsqueeze(2).to_broadcast([P, 2, 2, w]),
+                in1=f[2].unsqueeze(1).to_broadcast([P, 2, 2, w]),
                 op=MULT,
             )
-            a8 = factor_pool.tile([P, 4, 2, CHUNK], F32, name="a8")
+            a8 = product_pool.tile([P, 4, 2, w], F32, name="a8_%d" % n, bufs=5 - 2 * n)
             eng.tensor_tensor(
                 out=a8[:],
-                in0=a4[:].rearrange("p a b n -> p (a b) n").unsqueeze(2).to_broadcast([P, 4, 2, CHUNK]),
-                in1=factors[3][:].unsqueeze(1).to_broadcast([P, 4, 2, CHUNK]),
+                in0=a4[:].rearrange("p a b n -> p (a b) n").unsqueeze(2).to_broadcast([P, 4, 2, w]),
+                in1=f[3].unsqueeze(1).to_broadcast([P, 4, 2, w]),
                 op=MULT,
             )
-            upper[q] = a8[:].rearrange("p a b n -> p (a b) n")
-            lower[q] = c2
+            for k in range(n):
+                upper[t + k] = a8[:].rearrange("p a b n -> p (a b) n")[:, :, k * P : (k + 1) * P]
+                lower[t + k] = c2[:, :, k * P : (k + 1) * P]
 
         lower_banks = {}
 
         def copy_lower(t):
-            q, i = divmod(t, CHUNK_TILES)
-            lower_ps = psum.tile([P, P, PACK], F32, tag="lower_ps", bufs=3)
-            for b4 in range(2):
-                for b5 in range(2):
-                    nc.tensor.matmul(
-                        out=lower_ps[:, :, 2 * b4 + b5],
-                        lhsT=select[b4][:].rearrange("p h t -> p (h t)"),
-                        rhs=lower[q][:, b5, i * P : (i + 1) * P],
-                        start=True,
-                        stop=True,
-                    )
+            lower_ps = psum.tile([P, PACK, P], F32, tag="lower_ps", bufs=3)
+            for out_ap, matrix, rhs in (
+                (lower_ps[:, 0:2, :], ident, lower[t]),
+                (lower_ps[:, 2, :], swap, lower[t][:, 1, :]),
+                (lower_ps[:, 3, :], swap, lower[t][:, 0, :]),
+            ):
+                nc.tensor.matmul(out=out_ap, lhsT=matrix[:], rhs=rhs, start=True, stop=True)
             lower_banks[t] = lower_ps
 
         paths = {}
 
-        def lower_to_sbuf(t):
-            lower_sb = const.tile([P, P, PACK], F32)
-            nc.scalar.copy(out=lower_sb[:], in_=lower_banks[t][:])
-            lower_banks[t] = lower_sb
-
-        def multiply(t, eng):
-            q, i = divmod(t, CHUNK_TILES)
-            path = path_pool.tile([P, PASSES, P, PACK], BF16, align_bytes=64)
-            eng.tensor_tensor(
+        def multiply(t):
+            path = path_pool.tile([P, PASSES, P, PACK], BF16, align_bytes=64, name="path")
+            nc.vector.tensor_tensor(
                 out=path[:],
-                in0=upper[q][:, :, i * P : (i + 1) * P].unsqueeze(3).to_broadcast([P, PASSES, P, PACK]),
-                in1=lower_banks[t][:].unsqueeze(1).to_broadcast([P, PASSES, P, PACK]),
+                in0=upper[t].unsqueeze(3).to_broadcast([P, PASSES, P, PACK]),
+                in1=lower_banks[t][:].rearrange("p j n -> p n j").unsqueeze(1).to_broadcast([P, PASSES, P, PACK]),
                 op=MULT,
             )
             paths[t] = path
 
-        results = {}
+        logs = {}
 
-        def contract(t):
-            q, i = divmod(t, CHUNK_TILES)
-            path_codes = path_pool.tile([P, PASSES, P], U32, align_bytes=64)
-            path_scales = path_pool.tile([P, PASSES, P], U8, align_bytes=64)
+        def log_factor_steps(first, n):
+            planes = const.tile([P, DEPTH, n * P], F32, name="logs%d" % first)
+            for k in range(n):
+                logs[first + k] = (planes, slice(k * P, (k + 1) * P))
+            steps = []
+            for level in range(DEPTH):
+
+                def step(level=level):
+                    factor(planes[:, level, :], logits(level, first, n), level, 0)
+
+                steps.append(step)
+            return steps
+
+        def logarithm_steps(first):
+            planes = logs[first][0]
+            steps = []
+            for level in range(DEPTH):
+
+                def step(level=level):
+                    nc.scalar.activation(out=planes[:, level, :], in_=planes[:, level, :], func=LN, bias=floor[:])
+
+                steps.append(step)
+            return steps
+
+        def add_transposed(out_ap, parts):
+            for k, (part, matrix) in enumerate(parts):
+                nc.tensor.matmul(
+                    out=out_ap, lhsT=part, rhs=matrix[:], start=(k == 0), stop=(k == len(parts) - 1), is_transpose=True
+                )
+
+        sums = {}
+
+        def sum_steps(t):
+            planes, cols = logs[t]
+            steps = []
+            for k0 in range(0, PASSES + PACK, PACK):
+
+                def sum_step(k0=k0):
+                    if k0 == 0:
+                        sums[t] = scratch_pool.tile([P, PASSES + PACK, P], F32, tag="scratch", name="log_sums")
+                    bank = psum.tile([P, 4, P], F32, tag="x_t")
+                    for k in range(4):
+                        if k0 < PASSES:
+                            g = k0 + k
+                            bits = {0: 0, 1: g >> 2, 2: (g >> 1) & 1, 3: g & 1}
+                        else:
+                            bits = {4: k >> 1, 5: k & 1}
+                        parts = []
+                        for level in bits:
+                            parts.append((planes[:, level, cols], swap if bits[level] else ident))
+                        add_transposed(bank[:, k, :], parts)
+                    nc.scalar.copy(out=sums[t][:, k0 : k0 + 4, :], in_=bank[:])
+
+                steps.append(sum_step)
+            return steps
+
+        def exp_steps(t):
+            steps = []
+            for g in range(PASSES):
+
+                def exp_step(g=g):
+                    if g == 0:
+                        paths[t] = path_pool.tile(
+                            [P, PASSES, P, PACK], BF16, align_bytes=64, tag="log_path", bufs=LOG_PATHS, name="log_path"
+                        )
+                    bank = psum.tile([P, PACK, P], F32, tag="z")
+                    for j in range(PACK):
+                        add_transposed(bank[:, j, :], [(sums[t][:, g, :], ident), (sums[t][:, PASSES + j, :], ident)])
+                    nc.scalar.activation(out=paths[t][:, g, :, :], in_=bank[:].rearrange("p j n -> p n j"), func=EXP)
+
+                steps.append(exp_step)
+            return steps
+
+        codes = {}
+
+        def quantise(t):
+            path_codes = path_pool.tile([P, PASSES, P], U32, align_bytes=64, bufs=3, name="path_codes")
+            path_scales = path_pool.tile([P, PASSES, P], U8, align_bytes=64, bufs=3, name="path_scales")
             nc.vector.quantize_mx(
                 out=path_codes[:].rearrange("p g n -> p (g n)").bitcast(FP8X4),
                 scales=path_scales[:].rearrange("p g n -> p (g n)"),
                 in_=paths[t][:].rearrange("p g n j -> p (g n j)"),
             )
-            acc = psum.tile([P, D_OUT], F32, tag="acc", bufs=1)
+            codes[t] = (path_codes, path_scales)
+
+        accs = []
+
+        def contract(t, place):
+            path_codes, path_scales = codes[t]
+            if place == 0:
+                accs.append(psum.tile([P, CHUNK_TILES, D_OUT], F32, tag="acc", bufs=1, name="acc"))
             for g in range(PASSES):
                 nc.tensor.matmul_mx(
-                    out=acc[:],
+                    out=accs[-1][:, place, :],
                     lhsT=path_codes[:, g, :].bitcast(FP8X4),
                     lhsT_scale=path_scales[:, g, :],
                     rhs=leaf_codes[:, g, :].bitcast(FP8X4),
@@ -252,48 +354,94 @@ def tile_neuralobliviousdecisiontree_e_kernel(tc, x, W_words, W_scales, b, leaf_
                     start=(g == 0),
                     stop=(g == PASSES - 1),
                 )
-            if i == 0:
-                results[q] = out_pool.tile([P, CHUNK_TILES, D_OUT], F32, name="result")
-            nc.scalar.activation(out=results[q][:, i, :], in_=acc[:], func=COPY, scale=1.0 / TREES)
-            if i == CHUNK_TILES - 1:
-                nc.sync.dma_start(out=out_rows[:, q * CHUNK_TILES : (q + 1) * CHUNK_TILES, :], in_=results[q][:])
 
-        transpose_x(0)
+        def store(run, lo, hi):
+            result = out_pool.tile([P, CHUNK_TILES, D_OUT], F32, name="result")
+            nc.scalar.activation(out=result[:, lo:hi, :], in_=accs[-1][:, lo:hi, :], func=COPY, scale=1.0 / TREES)
+            for place in range(lo, hi):
+                nc.sync.dma_start(out=out_rows[:, run[place], :], in_=result[:, place, :])
+
+        zs = [None]
+
+        transpose_x(0, 0, nc.scalar.copy)
+        transpose_x(0, 1, nc.vector.tensor_copy)
         b_cols = psum.tile([P, P], F32, tag="x_t")
         nc.tensor.transpose(out=b_cols[:], in_=b_rows_f32[:], identity=ident[:])
-        bias_keep = const.tile([P, DEPTH], F32)
-        bias_flip = const.tile([P, DEPTH], F32)
-        half_bias = const.tile([P, DEPTH], F32)
-        nc.vector.tensor_copy(out=bias_keep[:], in_=b_cols[:, 0:DEPTH])
-        nc.vector.tensor_scalar_mul(out=bias_flip[:], in0=b_cols[:, 0:DEPTH], scalar1=-1.0)
-        nc.vector.tensor_scalar_mul(out=half_bias[:], in0=b_cols[:, 0:DEPTH], scalar1=half_sign[:, 0:1])
+        half_bias = const.tile([P, 2, DEPTH], F32)
+        for s in range(2):
+            nc.vector.tensor_scalar_mul(out=half_bias[:, s, :], in0=b_cols[:, 0:DEPTH], scalar1=half_sign[:, s : s + 1])
         quantise_x(0)
-        transpose_x(1)
-        quantise_x(1)
 
-        split_probabilities(0, nc.vector)
-        transpose_x(2)
-        quantise_x(2)
-        transpose_x(3)
-        quantise_x(3)
+        def do(step_list):
+            for step in step_list:
+                step()
+
+        def finish(run):
+            for place, t in enumerate(run):
+                quantise(t)
+                contract(t, place)
+
+
+        transpose_x(1, 0, nc.scalar.copy)
+        transpose_x(1, 1, nc.scalar.copy)
+        quantise_x(1)
+        do(factor_steps(0, 2))
+        prepare(0, 2, nc.vector)
         copy_lower(0)
         copy_lower(1)
-        split_probabilities(1, nc.gpsimd)
-        regroup_leaves()
-
-        for q in range(N_CHUNKS):
-            for i in range(CHUNK_TILES):
-                t = q * CHUNK_TILES + i
-                if t + 2 < N_TILES:
-                    copy_lower(t + 2)
-                if q == N_CHUNKS - 1 and i == 0:
-                    lower_to_sbuf(t)
-                    multiply(t, nc.gpsimd)
-                else:
-                    multiply(t, nc.vector)
-                if i == 1 and q + 2 < N_CHUNKS:
-                    split_probabilities(q + 2, nc.gpsimd)
-            if q == 0:
-                quantise_leaves()
-            for i in range(CHUNK_TILES):
-                contract(q * CHUNK_TILES + i)
+        multiply(0)
+        do(factor_steps(4, 4))
+        for t in (4, 5, 6, 7):
+            prepare(t, 1, nc.gpsimd)
+        multiply(1)
+        transpose_x(2, 0, nc.scalar.copy)
+        transpose_x(2, 1, nc.scalar.copy)
+        do(log_factor_steps(2, 2))
+        quantise_x(2)
+        do(factor_steps(8, 4))
+        do(logarithm_steps(2))
+        regroup_leaves(0, 4)
+        copy_lower(4)
+        multiply(4)
+        do(sum_steps(2))
+        do(sum_steps(3))
+        regroup_leaves(4, 8)
+        copy_lower(5)
+        multiply(5)
+        quantise_leaves()
+        finish([0, 1, 4, 5])
+        copy_lower(6)
+        multiply(6)
+        do(exp_steps(2))
+        store([0, 1, 4, 5], 0, 4)
+        for t in (8, 9, 10, 11):
+            prepare(t, 1, nc.gpsimd)
+        transpose_x(3, 0, nc.scalar.copy)
+        transpose_x(3, 1, nc.scalar.copy)
+        do(exp_steps(3))
+        copy_lower(7)
+        multiply(7)
+        quantise_x(3)
+        do(factor_steps(12, 2))
+        for t in [12,13]:
+            prepare(t, 1, nc.gpsimd)
+        finish([6, 7, 2, 3])
+        do(log_factor_steps(14, 2))
+        do(logarithm_steps(14))
+        store([6, 7, 2, 3], 0, 4)
+        for t in (8, 9, 10, 11):
+            copy_lower(t)
+            multiply(t)
+        finish([8, 9, 10, 11])
+        for t in [14,15]:
+            do(sum_steps(t))
+        do(exp_steps(14))
+        store([8, 9, 10, 11], 0, 4)
+        for t in [15]:
+            do(exp_steps(t))
+        for t in [12,13]:
+            copy_lower(t)
+            multiply(t)
+        finish([12, 13, 14, 15])
+        store([12, 13, 14, 15], 0, 3)
+        store([12, 13, 14, 15], 3, 4)

@@ -15,7 +15,6 @@ LN = mybir.ActivationFunctionType.Ln
 EXP = mybir.ActivationFunctionType.Exp
 COPY = mybir.ActivationFunctionType.Copy
 
-PINNED = {mybir.EngineType.Activation, mybir.EngineType.DVE, mybir.EngineType.Pool, mybir.EngineType.SP}
 P = 128
 PACK = 4
 BATCH, FEATURES, DEPTH, TREES, LEAVES, D_OUT = 2048, 512, 6, 64, 64, 128
@@ -24,7 +23,7 @@ N_TILES = BATCH // P
 CHUNK_TILES = 4
 CHUNK = CHUNK_TILES * P
 N_CHUNKS = N_TILES // CHUNK_TILES
-N_PRODUCT = 12
+N_PRODUCT = 13
 LEVEL_ORDER = (4, 5, 0, 1, 2, 3)
 HALF_LEVELS = (0, 4)
 LOG_PATHS = 4
@@ -35,7 +34,7 @@ FLOPS = 2 * BATCH * FEATURES * DEPTH * TREES + 2 * BATCH * TREES * LEAVES * D_OU
 def tile_neuralobliviousdecisiontree_e_kernel(tc, x, W_words, W_scales, b, leaf_values, out):
     nc = tc.nc
     with ExitStack() as ctx:
-        ctx.enter_context(tc.manual_schedule(engines=PINNED))
+        ctx.enter_context(tc.manual_schedule())
         const = ctx.enter_context(tc.tile_pool(name="const", bufs=1))
         x_pool = ctx.enter_context(tc.tile_pool(name="x_pool", bufs=3))
         factor_pool = ctx.enter_context(tc.tile_pool(name="factor_pool", bufs=2))
@@ -65,11 +64,11 @@ def tile_neuralobliviousdecisiontree_e_kernel(tc, x, W_words, W_scales, b, leaf_
         for b0 in range(2):
             nc.scalar.dma_start(out=b_rows[0:DEPTH, TREES * b0 : TREES * (b0 + 1)], in_=b)
         load_x(0, 0, 2)
-        load_x(0, 2, 4)
         nc.sync.dma_start(
             out=w_codes[:, :, 0, :].bitcast(I32),
             in_=W_words.rearrange("j p t e -> p j (t e)").bitcast(I32),
         )
+        load_x(0, 2, 4)
         scale_rows = W_scales.rearrange("j s t -> s j t").bitcast(I32)
         for quadrant in range(4):
             nc.sync.dma_start(
@@ -110,7 +109,7 @@ def tile_neuralobliviousdecisiontree_e_kernel(tc, x, W_words, W_scales, b, leaf_
         leaf_scales = const.tile([P, PASSES, D_OUT], U8, align_bytes=64)
 
         def regroup_leaves(lo, hi):
-            nc.vector.tensor_copy(
+            nc.scalar.copy(
                 out=leaf_grouped[:, lo:hi, :, :],
                 in_=leaf_raw[:, PACK * lo : PACK * hi, :].rearrange("p (g j) d -> p g d j", j=PACK),
             )
@@ -145,11 +144,17 @@ def tile_neuralobliviousdecisiontree_e_kernel(tc, x, W_words, W_scales, b, leaf_
                 in_=x_t[:].rearrange("p c u n -> p c n u"),
             )
 
-        def quantise_x(q):
-            x_codes = const.tile([P, CHUNK], U32, align_bytes=64, name="x_codes%d" % q)
-            x_scales = const.tile([P, CHUNK], U8, align_bytes=64, name="x_scales%d" % q)
-            nc.vector.quantize_mx(out=x_codes[:].bitcast(FP8X4), scales=x_scales[:], in_=x_grouped[q][:])
-            x_mx[q] = (x_codes, x_scales)
+        def quantise_x(q, lo, hi):
+            if lo == 0:
+                x_codes = const.tile([P, CHUNK], U32, align_bytes=64, name="x_codes%d" % q)
+                x_scales = const.tile([P, CHUNK], U8, align_bytes=64, name="x_scales%d" % q)
+                x_mx[q] = (x_codes, x_scales)
+            cols = slice(lo * P, hi * P)
+            nc.vector.quantize_mx(
+                out=x_mx[q][0][:, cols].bitcast(FP8X4),
+                scales=x_mx[q][1][:, cols],
+                in_=x_grouped[q][:, PACK * lo * P : PACK * hi * P],
+            )
 
         def logits(level, first, n):
             q, i = divmod(first, CHUNK_TILES)
@@ -174,6 +179,11 @@ def tile_neuralobliviousdecisiontree_e_kernel(tc, x, W_words, W_scales, b, leaf_
 
         factors = {}
 
+        def new_factor(q, level, bits):
+            if q < N_CHUNKS - 1:
+                return factor_pool.tile([P, bits, CHUNK], F32, name="f%d" % level)
+            return const.tile([P, bits, (N_PRODUCT - q * CHUNK_TILES) * P], F32, name="last_f%d" % level)
+
         def factor_steps(first, n):
             q, i = divmod(first, CHUNK_TILES)
             cols = slice(i * P, (i + n) * P)
@@ -183,7 +193,7 @@ def tile_neuralobliviousdecisiontree_e_kernel(tc, x, W_words, W_scales, b, leaf_
                 def step_0(level=level):
                     half = level in HALF_LEVELS
                     if (q, level) not in factors:
-                        factors[(q, level)] = factor_pool.tile([P, 1 if half else 2, CHUNK], F32, name="f%d" % level)
+                        factors[(q, level)] = new_factor(q, level, 1 if half else 2)
                     zs[0] = logits(level, first, n)
                     factor(factors[(q, level)][:, 0, cols], zs[0], level, 0)
 
@@ -198,34 +208,42 @@ def tile_neuralobliviousdecisiontree_e_kernel(tc, x, W_words, W_scales, b, leaf_
         upper = {}
         lower = {}
 
-        def prepare(t, n, eng):
+        def prepare_lower(t, n, eng):
             q, i = divmod(t, CHUNK_TILES)
             cols = slice(i * P, (i + n) * P)
-            f = []
-            for level in range(DEPTH):
-                f.append(factors[(q, level)][:, :, cols])
-            w = n * P
-            c2 = product_pool.tile([P, 2, w], F32, name="c2_%d" % n, bufs=4 - n)
-            eng.tensor_tensor(out=c2[:], in0=f[4].to_broadcast([P, 2, w]), in1=f[5], op=MULT)
-            a2 = product_pool.tile([P, 2, w], F32, name="a2_%d" % n, bufs=1)
-            eng.tensor_tensor(out=a2[:], in0=f[0].to_broadcast([P, 2, w]), in1=f[1], op=MULT)
-            a4 = product_pool.tile([P, 2, 2, w], F32, name="a4_%d" % n, bufs=1)
+            c2 = product_pool.tile([P, 2, CHUNK], F32, name="c2", bufs=2)
             eng.tensor_tensor(
-                out=a4[:],
-                in0=a2[:].unsqueeze(2).to_broadcast([P, 2, 2, w]),
-                in1=f[2].unsqueeze(1).to_broadcast([P, 2, 2, w]),
-                op=MULT,
-            )
-            a8 = product_pool.tile([P, 4, 2, w], F32, name="a8_%d" % n, bufs=5 - 2 * n)
-            eng.tensor_tensor(
-                out=a8[:],
-                in0=a4[:].rearrange("p a b n -> p (a b) n").unsqueeze(2).to_broadcast([P, 4, 2, w]),
-                in1=f[3].unsqueeze(1).to_broadcast([P, 4, 2, w]),
+                out=c2[:, :, 0 : n * P],
+                in0=factors[(q, 4)][:, :, cols].to_broadcast([P, 2, n * P]),
+                in1=factors[(q, 5)][:, :, cols],
                 op=MULT,
             )
             for k in range(n):
-                upper[t + k] = a8[:].rearrange("p a b n -> p (a b) n")[:, :, k * P : (k + 1) * P]
                 lower[t + k] = c2[:, :, k * P : (k + 1) * P]
+
+        def prepare_upper(t, eng):
+            q, i = divmod(t, CHUNK_TILES)
+            cols = slice(i * P, (i + 1) * P)
+            f = []
+            for level in range(4):
+                f.append(factors[(q, level)][:, :, cols])
+            a2 = product_pool.tile([P, 2, P], F32, name="a2", bufs=2)
+            eng.tensor_tensor(out=a2[:], in0=f[0].to_broadcast([P, 2, P]), in1=f[1], op=MULT)
+            a4 = product_pool.tile([P, 2, 2, P], F32, name="a4", bufs=2)
+            eng.tensor_tensor(
+                out=a4[:],
+                in0=a2[:].unsqueeze(2).to_broadcast([P, 2, 2, P]),
+                in1=f[2].unsqueeze(1).to_broadcast([P, 2, 2, P]),
+                op=MULT,
+            )
+            a8 = product_pool.tile([P, 4, 2, P], F32, name="a8")
+            eng.tensor_tensor(
+                out=a8[:],
+                in0=a4[:].rearrange("p a b n -> p (a b) n").unsqueeze(2).to_broadcast([P, 4, 2, P]),
+                in1=f[3].unsqueeze(1).to_broadcast([P, 4, 2, P]),
+                op=MULT,
+            )
+            upper[t] = a8[:].rearrange("p a b n -> p (a b) n")
 
         lower_banks = {}
 
@@ -329,8 +347,8 @@ def tile_neuralobliviousdecisiontree_e_kernel(tc, x, W_words, W_scales, b, leaf_
         codes = {}
 
         def quantise(t):
-            path_codes = path_pool.tile([P, PASSES, P], U32, align_bytes=64, bufs=3, name="path_codes")
-            path_scales = path_pool.tile([P, PASSES, P], U8, align_bytes=64, bufs=3, name="path_scales")
+            path_codes = path_pool.tile([P, PASSES, P], U32, align_bytes=64, bufs=4, name="path_codes")
+            path_scales = path_pool.tile([P, PASSES, P], U8, align_bytes=64, bufs=4, name="path_scales")
             nc.vector.quantize_mx(
                 out=path_codes[:].rearrange("p g n -> p (g n)").bitcast(FP8X4),
                 scales=path_scales[:].rearrange("p g n -> p (g n)"),
@@ -363,85 +381,121 @@ def tile_neuralobliviousdecisiontree_e_kernel(tc, x, W_words, W_scales, b, leaf_
 
         zs = [None]
 
-        transpose_x(0, 0, nc.scalar.copy)
-        transpose_x(0, 1, nc.vector.tensor_copy)
+        for k in range(4):
+            warm = psum.tile([P, P], F32, tag="z")
+            nc.tensor.matmul(out=warm[:], lhsT=ident[:], rhs=ident[:], start=True, stop=True)
         b_cols = psum.tile([P, P], F32, tag="x_t")
         nc.tensor.transpose(out=b_cols[:], in_=b_rows_f32[:], identity=ident[:])
         half_bias = const.tile([P, 2, DEPTH], F32)
         for s in range(2):
             nc.vector.tensor_scalar_mul(out=half_bias[:, s, :], in0=b_cols[:, 0:DEPTH], scalar1=half_sign[:, s : s + 1])
-        quantise_x(0)
-
+        transpose_x(0, 0, nc.scalar.copy)
+        quantise_x(0, 0, 2)
         def do(step_list):
             for step in step_list:
                 step()
 
-        def finish(run):
+        def weave(*step_lists):
+            marked = []
+            for n, step_list in enumerate(step_lists):
+                for k, step in enumerate(step_list):
+                    marked.append(((k + 0.5) / len(step_list), n, k, step))
+            for mark in sorted(marked, key=lambda mark: mark[0:3]):
+                mark[3]()
+
+        def finish_steps(run):
+            steps = []
             for place, t in enumerate(run):
-                quantise(t)
-                contract(t, place)
 
+                def step(place=place, t=t):
+                    quantise(t)
+                    contract(t, place)
 
-        transpose_x(1, 0, nc.scalar.copy)
-        transpose_x(1, 1, nc.scalar.copy)
-        quantise_x(1)
-        do(factor_steps(0, 2))
-        prepare(0, 2, nc.vector)
+                steps.append(step)
+            return steps
+
+        firsts = factor_steps(0, 2)
+        do(firsts[0:3])
+        transpose_x(0, 1, nc.vector.tensor_copy)
+        quantise_x(0, 2, 4)
+        prepare_lower(0, 2, nc.vector)
+        do(firsts[3:])
+        prepare_upper(0, nc.vector)
         copy_lower(0)
+        prepare_upper(1, nc.gpsimd)
+        seconds = factor_steps(2, 2)
+        do(seconds[0:3])
         copy_lower(1)
+        prepare_lower(2, 2, nc.gpsimd)
+        do(seconds[3:])
+        for pair in range(2):
+            transpose_x(1, pair, nc.scalar.copy)
         multiply(0)
-        do(factor_steps(4, 4))
+        quantise_x(1, 0, 4)
+        for t in (2, 3):
+            prepare_upper(t, nc.gpsimd)
+        for q in (2, 3):
+            for pair in range(2):
+                transpose_x(q, pair, nc.scalar.copy)
+        fours = factor_steps(4, 4)
+        do(fours[0:5])
+        copy_lower(2)
+        do(fours[5:])
+        prepare_lower(4, 4, nc.gpsimd)
         for t in (4, 5, 6, 7):
-            prepare(t, 1, nc.gpsimd)
+            prepare_upper(t, nc.gpsimd)
         multiply(1)
-        transpose_x(2, 0, nc.scalar.copy)
-        transpose_x(2, 1, nc.scalar.copy)
-        do(log_factor_steps(2, 2))
-        quantise_x(2)
+        regroup_leaves(0, 8)
+        copy_lower(3)
+        multiply(2)
+        quantise_x(2, 0, 4)
+        quantise_x(3, 0, 4)
         do(factor_steps(8, 4))
-        do(logarithm_steps(2))
-        regroup_leaves(0, 4)
         copy_lower(4)
-        multiply(4)
-        do(sum_steps(2))
-        do(sum_steps(3))
-        regroup_leaves(4, 8)
-        copy_lower(5)
-        multiply(5)
+        multiply(3)
+        do(factor_steps(12, 1))
         quantise_leaves()
-        finish([0, 1, 4, 5])
-        copy_lower(6)
-        multiply(6)
-        do(exp_steps(2))
-        store([0, 1, 4, 5], 0, 4)
-        for t in (8, 9, 10, 11):
-            prepare(t, 1, nc.gpsimd)
-        transpose_x(3, 0, nc.scalar.copy)
-        transpose_x(3, 1, nc.scalar.copy)
-        do(exp_steps(3))
-        copy_lower(7)
-        multiply(7)
-        quantise_x(3)
-        do(factor_steps(12, 2))
-        for t in [12,13]:
-            prepare(t, 1, nc.gpsimd)
-        finish([6, 7, 2, 3])
+        do(log_factor_steps(13, 1))
         do(log_factor_steps(14, 2))
+        do(finish_steps([0, 1, 2, 3]))
+        copy_lower(5)
+        do(logarithm_steps(13))
         do(logarithm_steps(14))
-        store([6, 7, 2, 3], 0, 4)
+        work = []
+        for t in (13, 14, 15):
+            work.extend(sum_steps(t))
+        for t in (13, 14, 15):
+            work.extend(exp_steps(t))
+        multiply(4)
+        store([0, 1, 2, 3], 0, 4)
+        copy_lower(6)
+        do(work[0:3])
+        prepare_lower(8, 4, nc.gpsimd)
         for t in (8, 9, 10, 11):
-            copy_lower(t)
+            prepare_upper(t, nc.gpsimd)
+        prepare_lower(12, 1, nc.gpsimd)
+        prepare_upper(12, nc.gpsimd)
+        multiply(5)
+        copy_lower(7)
+        do(work[3:6])
+        multiply(6)
+        copy_lower(8)
+        do(work[6:9])
+        multiply(7)
+        copy_lower(9)
+        do(work[9:13])
+        do(finish_steps([4, 5, 6, 7]))
+        for t in (8, 9, 10, 11):
             multiply(t)
-        finish([8, 9, 10, 11])
-        for t in [14,15]:
-            do(sum_steps(t))
-        do(exp_steps(14))
+            if t + 2 < 13:
+                copy_lower(t + 2)
+            k = 13 + 5 * (t - 8)
+            do(work[k : k + 5])
+            if t == 8:
+                store([4, 5, 6, 7], 0, 4)
+        do(finish_steps([8, 9, 10, 11]))
+        multiply(12)
         store([8, 9, 10, 11], 0, 4)
-        for t in [15]:
-            do(exp_steps(t))
-        for t in [12,13]:
-            copy_lower(t)
-            multiply(t)
-        finish([12, 13, 14, 15])
-        store([12, 13, 14, 15], 0, 3)
-        store([12, 13, 14, 15], 3, 4)
+        do(finish_steps([13, 14, 15, 12]))
+        store([13, 14, 15, 12], 0, 3)
+        store([13, 14, 15, 12], 3, 4)

@@ -121,6 +121,10 @@ def tile_neuralobliviousdecisiontree_e_kernel(tc, x, W_words, W_scales, b, leaf_
                 in_=leaf_grouped[:].rearrange("p g d j -> p (g d j)"),
             )
 
+        def do(step_list):
+            for step in step_list:
+                step()
+
         x_grouped = {}
         x_mx = {}
 
@@ -247,15 +251,21 @@ def tile_neuralobliviousdecisiontree_e_kernel(tc, x, W_words, W_scales, b, leaf_
 
         lower_banks = {}
 
+        def copy_lower_steps(t):
+            def step_0():
+                lower_banks[t] = psum.tile([P, PACK, P], F32, tag="lower_ps", bufs=3, name="lower_ps")
+                nc.tensor.matmul(out=lower_banks[t][:, 0:2, :], lhsT=ident[:], rhs=lower[t], start=True, stop=True)
+
+            def step_1():
+                for j in (2, 3):
+                    nc.tensor.matmul(
+                        out=lower_banks[t][:, j, :], lhsT=swap[:], rhs=lower[t][:, 3 - j, :], start=True, stop=True
+                    )
+
+            return [step_0, step_1]
+
         def copy_lower(t):
-            lower_ps = psum.tile([P, PACK, P], F32, tag="lower_ps", bufs=3)
-            for out_ap, matrix, rhs in (
-                (lower_ps[:, 0:2, :], ident, lower[t]),
-                (lower_ps[:, 2, :], swap, lower[t][:, 1, :]),
-                (lower_ps[:, 3, :], swap, lower[t][:, 0, :]),
-            ):
-                nc.tensor.matmul(out=out_ap, lhsT=matrix[:], rhs=rhs, start=True, stop=True)
-            lower_banks[t] = lower_ps
+            do(copy_lower_steps(t))
 
         paths = {}
 
@@ -391,10 +401,6 @@ def tile_neuralobliviousdecisiontree_e_kernel(tc, x, W_words, W_scales, b, leaf_
             nc.vector.tensor_scalar_mul(out=half_bias[:, s, :], in0=b_cols[:, 0:DEPTH], scalar1=half_sign[:, s : s + 1])
         transpose_x(0, 0, nc.scalar.copy)
         quantise_x(0, 0, 2)
-        def do(step_list):
-            for step in step_list:
-                step()
-
         def weave(*step_lists):
             marked = []
             for n, step_list in enumerate(step_lists):
@@ -468,29 +474,23 @@ def tile_neuralobliviousdecisiontree_e_kernel(tc, x, W_words, W_scales, b, leaf_
             work.extend(exp_steps(t))
         multiply(4)
         store([0, 1, 2, 3], 0, 4)
-        copy_lower(6)
-        do(work[0:3])
+        weave(work[0:3], copy_lower_steps(6))
         prepare_lower(8, 4, nc.gpsimd)
         for t in (8, 9, 10, 11):
             prepare_upper(t, nc.gpsimd)
         prepare_lower(12, 1, nc.gpsimd)
         prepare_upper(12, nc.gpsimd)
         multiply(5)
-        copy_lower(7)
-        do(work[3:6])
+        weave(work[3:6], copy_lower_steps(7))
         multiply(6)
-        copy_lower(8)
-        do(work[6:9])
+        weave(work[6:9], copy_lower_steps(8))
         multiply(7)
-        copy_lower(9)
-        do(work[9:13])
+        weave(work[9:13], copy_lower_steps(9))
         do(finish_steps([4, 5, 6, 7]))
         for t in (8, 9, 10, 11):
             multiply(t)
-            if t + 2 < 13:
-                copy_lower(t + 2)
             k = 13 + 5 * (t - 8)
-            do(work[k : k + 5])
+            weave(work[k : k + 5], copy_lower_steps(t + 2) if t + 2 < 13 else [])
             if t == 8:
                 store([4, 5, 6, 7], 0, 4)
         do(finish_steps([8, 9, 10, 11]))

@@ -23,7 +23,7 @@ N_TILES = BATCH // P
 CHUNK_TILES = 4
 CHUNK = CHUNK_TILES * P
 N_CHUNKS = N_TILES // CHUNK_TILES
-N_PRODUCT = 13
+N_PRODUCT = 12
 LEVEL_ORDER = (4, 5, 0, 1, 2, 3)
 HALF_LEVELS = (0, 4)
 LOG_PATHS = 4
@@ -184,9 +184,7 @@ def tile_neuralobliviousdecisiontree_e_kernel(tc, x, W_words, W_scales, b, leaf_
         factors = {}
 
         def new_factor(q, level, bits):
-            if q < N_CHUNKS - 1:
-                return factor_pool.tile([P, bits, CHUNK], F32, name="f%d" % level)
-            return const.tile([P, bits, (N_PRODUCT - q * CHUNK_TILES) * P], F32, name="last_f%d" % level)
+            return factor_pool.tile([P, bits, CHUNK], F32, name="f%d" % level)
 
         def factor_steps(first, n):
             q, i = divmod(first, CHUNK_TILES)
@@ -282,27 +280,45 @@ def tile_neuralobliviousdecisiontree_e_kernel(tc, x, W_words, W_scales, b, leaf_
         logs = {}
 
         def log_factor_steps(first, n):
-            planes = const.tile([P, DEPTH, n * P], F32, name="logs%d" % first)
+            firsts = const.tile([P, DEPTH // 2, n * P], F32, name="log_firsts")
+            pairs = const.tile([P, DEPTH // 2, 2, n * P], F32, name="log_pairs")
             for k in range(n):
-                logs[first + k] = (planes, slice(k * P, (k + 1) * P))
+                logs[first + k] = (firsts, pairs, slice(k * P, (k + 1) * P))
             steps = []
             for level in range(DEPTH):
 
                 def step(level=level):
-                    factor(planes[:, level, :], logits(level, first, n), level, 0)
+                    z = logits(level, first, n)
+                    if level % 2 == 0:
+                        factor(firsts[:, level // 2, :], z, level, 0)
+                    else:
+                        for s in range(2):
+                            factor(pairs[:, level // 2, s, :], z, level, s)
 
                 steps.append(step)
             return steps
 
+        def multiply_pairs(first, pair):
+            firsts, pairs, cols = logs[first]
+            nc.vector.tensor_tensor(
+                out=pairs[:, pair, :, :],
+                in0=firsts[:, pair : pair + 1, :].to_broadcast([P, 2, firsts.shape[2]]),
+                in1=pairs[:, pair, :, :],
+                op=MULT,
+            )
+
         def logarithm_steps(first):
-            planes = logs[first][0]
+            pairs = logs[first][1]
             steps = []
-            for level in range(DEPTH):
+            for pair in range(DEPTH // 2):
+                for s in range(2):
 
-                def step(level=level):
-                    nc.scalar.activation(out=planes[:, level, :], in_=planes[:, level, :], func=LN, bias=floor[:])
+                    def step(pair=pair, s=s):
+                        nc.scalar.activation(
+                            out=pairs[:, pair, s, :], in_=pairs[:, pair, s, :], func=LN, bias=floor[:]
+                        )
 
-                steps.append(step)
+                    steps.append(step)
             return steps
 
         def add_transposed(out_ap, parts):
@@ -314,7 +330,11 @@ def tile_neuralobliviousdecisiontree_e_kernel(tc, x, W_words, W_scales, b, leaf_
         sums = {}
 
         def sum_steps(t):
-            planes, cols = logs[t]
+            pairs, cols = logs[t][1:]
+
+            def pair_sum(pair, bit, next_bit):
+                return (pairs[:, pair, bit ^ next_bit, cols], swap if bit else ident)
+
             steps = []
             for k0 in range(0, PASSES + PACK, PACK):
 
@@ -325,12 +345,9 @@ def tile_neuralobliviousdecisiontree_e_kernel(tc, x, W_words, W_scales, b, leaf_
                     for k in range(4):
                         if k0 < PASSES:
                             g = k0 + k
-                            bits = {0: 0, 1: g >> 2, 2: (g >> 1) & 1, 3: g & 1}
+                            parts = [pair_sum(0, 0, g >> 2), pair_sum(1, (g >> 1) & 1, g & 1)]
                         else:
-                            bits = {4: k >> 1, 5: k & 1}
-                        parts = []
-                        for level in bits:
-                            parts.append((planes[:, level, cols], swap if bits[level] else ident))
+                            parts = [pair_sum(2, k >> 1, k & 1)]
                         add_transposed(bank[:, k, :], parts)
                     nc.scalar.copy(out=sums[t][:, k0 : k0 + 4, :], in_=bank[:])
 
@@ -346,7 +363,7 @@ def tile_neuralobliviousdecisiontree_e_kernel(tc, x, W_words, W_scales, b, leaf_
                         paths[t] = path_pool.tile(
                             [P, PASSES, P, PACK], BF16, align_bytes=64, tag="log_path", bufs=LOG_PATHS, name="log_path"
                         )
-                    bank = psum.tile([P, PACK, P], F32, tag="z")
+                    bank = psum.tile([P, PACK, P], F32, tag="z" if g % 2 == 0 else "x_t")
                     for j in range(PACK):
                         add_transposed(bank[:, j, :], [(sums[t][:, g, :], ident), (sums[t][:, PASSES + j, :], ident)])
                     nc.scalar.activation(out=paths[t][:, g, :, :], in_=bank[:].rearrange("p j n -> p n j"), func=EXP)
@@ -422,9 +439,9 @@ def tile_neuralobliviousdecisiontree_e_kernel(tc, x, W_words, W_scales, b, leaf_
 
         firsts = factor_steps(0, 2)
         do(firsts[0:3])
+        prepare_lower(0, 2, nc.vector)
         transpose_x(0, 1, nc.vector.tensor_copy)
         quantise_x(0, 2, 4)
-        prepare_lower(0, 2, nc.vector)
         do(firsts[3:])
         prepare_upper(0, nc.vector)
         copy_lower(0)
@@ -436,66 +453,70 @@ def tile_neuralobliviousdecisiontree_e_kernel(tc, x, W_words, W_scales, b, leaf_
         do(seconds[3:])
         for pair in range(2):
             transpose_x(1, pair, nc.scalar.copy)
+        regroup_leaves(0, 4)
         multiply(0)
         quantise_x(1, 0, 4)
         for t in (2, 3):
             prepare_upper(t, nc.gpsimd)
-        for q in (2, 3):
+        later_x = []
+        for q in (3, 2):
             for pair in range(2):
-                transpose_x(q, pair, nc.scalar.copy)
+                later_x.append(lambda q=q, pair=pair: transpose_x(q, pair, nc.scalar.copy))
         fours = factor_steps(4, 4)
-        do(fours[0:5])
         copy_lower(2)
-        do(fours[5:])
+        weave(fours[0:5], later_x[0:2])
+        weave(fours[5:], later_x[2:4])
         prepare_lower(4, 4, nc.gpsimd)
         for t in (4, 5, 6, 7):
             prepare_upper(t, nc.gpsimd)
         multiply(1)
-        regroup_leaves(0, 8)
+        regroup_leaves(4, 8)
         copy_lower(3)
         multiply(2)
-        quantise_x(2, 0, 4)
         quantise_x(3, 0, 4)
-        do(factor_steps(8, 4))
+        quantise_x(2, 0, 4)
+        do(log_factor_steps(12, 4))
         copy_lower(4)
         multiply(3)
-        do(factor_steps(12, 1))
         quantise_leaves()
-        do(log_factor_steps(13, 1))
-        do(log_factor_steps(14, 2))
-        do(finish_steps([0, 1, 2, 3]))
-        copy_lower(5)
-        do(logarithm_steps(13))
-        do(logarithm_steps(14))
+        for pair in range(DEPTH // 2):
+            multiply_pairs(12, pair)
+        do(logarithm_steps(12))
         work = []
-        for t in (13, 14, 15):
-            work.extend(sum_steps(t))
-        for t in (13, 14, 15):
-            work.extend(exp_steps(t))
-        multiply(4)
-        store([0, 1, 2, 3], 0, 4)
-        weave(work[0:3], copy_lower_steps(6))
-        prepare_lower(8, 4, nc.gpsimd)
-        for t in (8, 9, 10, 11):
-            prepare_upper(t, nc.gpsimd)
-        prepare_lower(12, 1, nc.gpsimd)
-        prepare_upper(12, nc.gpsimd)
-        multiply(5)
-        weave(work[3:6], copy_lower_steps(7))
-        multiply(6)
-        weave(work[6:9], copy_lower_steps(8))
-        multiply(7)
-        weave(work[9:13], copy_lower_steps(9))
-        do(finish_steps([4, 5, 6, 7]))
-        for t in (8, 9, 10, 11):
+        work.extend(sum_steps(12))
+        work.extend(sum_steps(13))
+        work.extend(exp_steps(12))
+        work.extend(sum_steps(14))
+        work.extend(exp_steps(13))
+        work.extend(sum_steps(15))
+        work.extend(exp_steps(14))
+        work.extend(exp_steps(15))
+        eights = factor_steps(8, 4)
+        copy_lower(5)
+        weave(eights, work[0:4])
+        for t in (0, 1, 2, 3):
+            quantise(t)
+        runs = {4: [0, 1, 2, 3], 7: [4, 5, 6, 7], 10: [8, 9, 10, 12]}
+        done = 4
+        for t in range(4, N_PRODUCT):
             multiply(t)
-            k = 13 + 5 * (t - 8)
-            weave(work[k : k + 5], copy_lower_steps(t + 2) if t + 2 < 13 else [])
-            if t == 8:
-                store([4, 5, 6, 7], 0, 4)
-        do(finish_steps([8, 9, 10, 11]))
-        multiply(12)
-        store([8, 9, 10, 11], 0, 4)
-        do(finish_steps([13, 14, 15, 12]))
-        store([13, 14, 15, 12], 0, 3)
-        store([13, 14, 15, 12], 3, 4)
+            if t + 2 < N_PRODUCT:
+                copy_lower(t + 2)
+            upto = 4 + (len(work) - 4) * min(t - 3, 7) // 7
+            do(work[done:upto])
+            done = upto
+            if t == 5:
+                prepare_lower(8, 4, nc.gpsimd)
+                for k in (8, 9, 10, 11):
+                    prepare_upper(k, nc.gpsimd)
+            if t in runs:
+                if t == 4:
+                    for place in range(4):
+                        contract(place, place)
+                else:
+                    do(finish_steps(runs[t]))
+                store(runs[t], 0, 4)
+        last = [13, 14, 15, 11]
+        do(finish_steps(last))
+        store(last, 0, 3)
+        store(last, 3, 4)

@@ -223,29 +223,49 @@ def tile_neuralobliviousdecisiontree_e_kernel(tc, x, W_words, W_scales, b, leaf_
             for k in range(n):
                 lower[t + k] = c2[:, :, k * P : (k + 1) * P]
 
-        def prepare_upper(t, eng):
+        partial = {}
+
+        def prepare_a2(t, n, eng):
             q, i = divmod(t, CHUNK_TILES)
-            cols = slice(i * P, (i + 1) * P)
-            f = []
-            for level in range(4):
-                f.append(factors[(q, level)][:, :, cols])
-            a2 = product_pool.tile([P, 2, P], F32, name="a2", bufs=2)
-            eng.tensor_tensor(out=a2[:], in0=f[0].to_broadcast([P, 2, P]), in1=f[1], op=MULT)
-            a4 = product_pool.tile([P, 2, 2, P], F32, name="a4", bufs=2)
+            cols = slice(i * P, (i + n) * P)
+            a2 = product_pool.tile([P, 2, CHUNK], F32, name="a2", bufs=1)
             eng.tensor_tensor(
-                out=a4[:],
-                in0=a2[:].unsqueeze(2).to_broadcast([P, 2, 2, P]),
-                in1=f[2].unsqueeze(1).to_broadcast([P, 2, 2, P]),
+                out=a2[:, :, 0 : n * P],
+                in0=factors[(q, 0)][:, :, cols].to_broadcast([P, 2, n * P]),
+                in1=factors[(q, 1)][:, :, cols],
                 op=MULT,
             )
-            a8 = product_pool.tile([P, 4, 2, P], F32, name="a8")
+            for k in range(n):
+                partial[("a2", t + k)] = (a2, k)
+
+        def prepare_a4(t, n, eng):
+            q, i = divmod(t, CHUNK_TILES)
+            a2, k0 = partial[("a2", t)]
+            a4 = product_pool.tile([P, 2, 2, 2 * P], F32, name="a4", bufs=1)
             eng.tensor_tensor(
-                out=a8[:],
-                in0=a4[:].rearrange("p a b n -> p (a b) n").unsqueeze(2).to_broadcast([P, 4, 2, P]),
-                in1=f[3].unsqueeze(1).to_broadcast([P, 4, 2, P]),
+                out=a4[:, :, :, 0 : n * P],
+                in0=a2[:, :, k0 * P : (k0 + n) * P].unsqueeze(2).to_broadcast([P, 2, 2, n * P]),
+                in1=factors[(q, 2)][:, :, i * P : (i + n) * P].unsqueeze(1).to_broadcast([P, 2, 2, n * P]),
                 op=MULT,
             )
-            upper[t] = a8[:].rearrange("p a b n -> p (a b) n")
+            for k in range(n):
+                partial[("a4", t + k)] = (a4, k)
+
+        def prepare_a8(t, n, eng):
+            q, i = divmod(t, CHUNK_TILES)
+            a4, k0 = partial[("a4", t)]
+            a8 = product_pool.tile([P, 4, 2, 1 * P], F32, name="a8", bufs=3)
+            eng.tensor_tensor(
+                out=a8[:, :, :, 0 : n * P],
+                in0=a4[:, :, :, k0 * P : (k0 + n) * P]
+                .rearrange("p a b n -> p (a b) n")
+                .unsqueeze(2)
+                .to_broadcast([P, 4, 2, n * P]),
+                in1=factors[(q, 3)][:, :, i * P : (i + n) * P].unsqueeze(1).to_broadcast([P, 4, 2, n * P]),
+                op=MULT,
+            )
+            for k in range(n):
+                upper[t + k] = a8[:].rearrange("p a b n -> p (a b) n")[:, :, k * P : (k + 1) * P]
 
         lower_banks = {}
 
@@ -443,9 +463,11 @@ def tile_neuralobliviousdecisiontree_e_kernel(tc, x, W_words, W_scales, b, leaf_
         transpose_x(0, 1, nc.vector.tensor_copy)
         quantise_x(0, 2, 4)
         do(firsts[3:])
-        prepare_upper(0, nc.vector)
+        prepare_a2(0, 2, nc.vector)
+        prepare_a4(0, 2, nc.vector)
+        prepare_a8(0, 1, nc.vector)
         copy_lower(0)
-        prepare_upper(1, nc.gpsimd)
+        prepare_a8(1, 1, nc.vector)
         seconds = factor_steps(2, 2)
         do(seconds[0:3])
         copy_lower(1)
@@ -456,8 +478,10 @@ def tile_neuralobliviousdecisiontree_e_kernel(tc, x, W_words, W_scales, b, leaf_
         regroup_leaves(0, 4)
         multiply(0)
         quantise_x(1, 0, 4)
+        prepare_a2(2, 2, nc.gpsimd)
+        prepare_a4(2, 2, nc.gpsimd)
         for t in (2, 3):
-            prepare_upper(t, nc.gpsimd)
+            prepare_a8(t, 1, nc.gpsimd)
         later_x = []
         for q in (3, 2):
             for pair in range(2):
@@ -466,13 +490,18 @@ def tile_neuralobliviousdecisiontree_e_kernel(tc, x, W_words, W_scales, b, leaf_
         copy_lower(2)
         weave(fours[0:5], later_x[0:2])
         weave(fours[5:], later_x[2:4])
-        prepare_lower(4, 4, nc.gpsimd)
-        for t in (4, 5, 6, 7):
-            prepare_upper(t, nc.gpsimd)
         multiply(1)
         regroup_leaves(4, 8)
         copy_lower(3)
         multiply(2)
+        prepare_lower(4, 4, nc.vector)
+        prepare_a2(4, 4, nc.gpsimd)
+        prepare_a4(4, 2, nc.gpsimd)
+        prepare_a8(4, 1, nc.gpsimd)
+        prepare_a8(5, 1, nc.gpsimd)
+        prepare_a4(6, 2, nc.gpsimd)
+        prepare_a8(6, 1, nc.gpsimd)
+        prepare_a8(7, 1, nc.gpsimd)
         quantise_x(3, 0, 4)
         quantise_x(2, 0, 4)
         do(log_factor_steps(12, 4))
@@ -483,8 +512,8 @@ def tile_neuralobliviousdecisiontree_e_kernel(tc, x, W_words, W_scales, b, leaf_
             multiply_pairs(12, pair)
         do(logarithm_steps(12))
         work = []
-        work.extend(sum_steps(12))
-        work.extend(sum_steps(13))
+        for t in (12, 13):
+            work.extend(sum_steps(t))
         work.extend(exp_steps(12))
         work.extend(sum_steps(14))
         work.extend(exp_steps(13))
@@ -507,8 +536,13 @@ def tile_neuralobliviousdecisiontree_e_kernel(tc, x, W_words, W_scales, b, leaf_
             done = upto
             if t == 5:
                 prepare_lower(8, 4, nc.gpsimd)
-                for k in (8, 9, 10, 11):
-                    prepare_upper(k, nc.gpsimd)
+                prepare_a2(8, 4, nc.gpsimd)
+                prepare_a4(8, 2, nc.gpsimd)
+                prepare_a8(8, 1, nc.gpsimd)
+                prepare_a8(9, 1, nc.gpsimd)
+                prepare_a4(10, 2, nc.gpsimd)
+                prepare_a8(10, 1, nc.gpsimd)
+                prepare_a8(11, 1, nc.gpsimd)
             if t in runs:
                 if t == 4:
                     for place in range(4):

@@ -312,7 +312,7 @@ def tile_neuralobliviousdecisiontree_e_kernel(tc, x, W_words, W_scales, b, leaf_
                     if level % 2 == 0:
                         factor(firsts[:, level // 2, :], z, level, 0)
                     else:
-                        for s in range(2):
+                        for s in range(2 if level // 2 in (0, 1) else 1):
                             factor(pairs[:, level // 2, s, :], z, level, s)
 
                 steps.append(step)
@@ -328,17 +328,20 @@ def tile_neuralobliviousdecisiontree_e_kernel(tc, x, W_words, W_scales, b, leaf_
             )
 
         def logarithm_steps(first):
-            pairs = logs[first][1]
-            steps = []
+            firsts, pairs, cols = logs[first]
+            planes = []
             for pair in range(DEPTH // 2):
-                for s in range(2):
+                if pair in (0, 1):
+                    planes.extend([pairs[:, pair, 0, :], pairs[:, pair, 1, :]])
+                else:
+                    planes.extend([firsts[:, pair, :], pairs[:, pair, 0, :]])
+            steps = []
+            for plane in planes:
 
-                    def step(pair=pair, s=s):
-                        nc.scalar.activation(
-                            out=pairs[:, pair, s, :], in_=pairs[:, pair, s, :], func=LN, bias=floor[:]
-                        )
+                def step(plane=plane):
+                    nc.scalar.activation(out=plane, in_=plane, func=LN, bias=floor[:])
 
-                    steps.append(step)
+                steps.append(step)
             return steps
 
         def add_transposed(out_ap, parts):
@@ -350,10 +353,12 @@ def tile_neuralobliviousdecisiontree_e_kernel(tc, x, W_words, W_scales, b, leaf_
         sums = {}
 
         def sum_steps(t):
-            pairs, cols = logs[t][1:]
+            firsts, pairs, cols = logs[t]
 
             def pair_sum(pair, bit, next_bit):
-                return (pairs[:, pair, bit ^ next_bit, cols], swap if bit else ident)
+                if pair in (0, 1):
+                    return [(pairs[:, pair, bit ^ next_bit, cols], swap if bit else ident)]
+                return [(firsts[:, pair, cols], swap if bit else ident), (pairs[:, pair, 0, cols], swap if next_bit else ident)]
 
             steps = []
             for k0 in range(0, PASSES + PACK, PACK):
@@ -365,9 +370,9 @@ def tile_neuralobliviousdecisiontree_e_kernel(tc, x, W_words, W_scales, b, leaf_
                     for k in range(4):
                         if k0 < PASSES:
                             g = k0 + k
-                            parts = [pair_sum(0, 0, g >> 2), pair_sum(1, (g >> 1) & 1, g & 1)]
+                            parts = pair_sum(0, 0, g >> 2) + pair_sum(1, (g >> 1) & 1, g & 1)
                         else:
-                            parts = [pair_sum(2, k >> 1, k & 1)]
+                            parts = pair_sum(2, k >> 1, k & 1)
                         add_transposed(bank[:, k, :], parts)
                     nc.scalar.copy(out=sums[t][:, k0 : k0 + 4, :], in_=bank[:])
 
@@ -384,6 +389,8 @@ def tile_neuralobliviousdecisiontree_e_kernel(tc, x, W_words, W_scales, b, leaf_
                             [P, PASSES, P, PACK], BF16, align_bytes=64, tag="log_path", bufs=LOG_PATHS, name="log_path"
                         )
                     bank = psum.tile([P, PACK, P], F32, tag="z" if g % 2 == 0 else "x_t")
+                    if g % 3 == 0:
+                        nc.tensor.matmul(out=bank[:, 0, 0:128], lhsT=ident[:], rhs=ident[:, 0:128], start=True, stop=True)
                     for j in range(PACK):
                         add_transposed(bank[:, j, :], [(sums[t][:, g, :], ident), (sums[t][:, PASSES + j, :], ident)])
                     nc.scalar.activation(out=paths[t][:, g, :, :], in_=bank[:].rearrange("p j n -> p n j"), func=EXP)
@@ -467,7 +474,7 @@ def tile_neuralobliviousdecisiontree_e_kernel(tc, x, W_words, W_scales, b, leaf_
         prepare_a4(0, 2, nc.vector)
         prepare_a8(0, 1, nc.vector)
         copy_lower(0)
-        prepare_a8(1, 1, nc.vector)
+        prepare_a8(1, 1, nc.gpsimd)
         seconds = factor_steps(2, 2)
         do(seconds[0:3])
         copy_lower(1)
@@ -490,11 +497,7 @@ def tile_neuralobliviousdecisiontree_e_kernel(tc, x, W_words, W_scales, b, leaf_
         copy_lower(2)
         weave(fours[0:5], later_x[0:2])
         weave(fours[5:], later_x[2:4])
-        multiply(1)
-        regroup_leaves(4, 8)
-        copy_lower(3)
-        multiply(2)
-        prepare_lower(4, 4, nc.vector)
+        prepare_lower(4, 4, nc.gpsimd)
         prepare_a2(4, 4, nc.gpsimd)
         prepare_a4(4, 2, nc.gpsimd)
         prepare_a8(4, 1, nc.gpsimd)
@@ -502,13 +505,17 @@ def tile_neuralobliviousdecisiontree_e_kernel(tc, x, W_words, W_scales, b, leaf_
         prepare_a4(6, 2, nc.gpsimd)
         prepare_a8(6, 1, nc.gpsimd)
         prepare_a8(7, 1, nc.gpsimd)
+        multiply(1)
+        regroup_leaves(4, 8)
+        copy_lower(3)
+        multiply(2)
         quantise_x(3, 0, 4)
         quantise_x(2, 0, 4)
         do(log_factor_steps(12, 4))
         copy_lower(4)
         multiply(3)
         quantise_leaves()
-        for pair in range(DEPTH // 2):
+        for pair in (0, 1):
             multiply_pairs(12, pair)
         do(logarithm_steps(12))
         work = []

@@ -312,7 +312,7 @@ def tile_neuralobliviousdecisiontree_e_kernel(tc, x, W_words, W_scales, b, leaf_
                     if level % 2 == 0:
                         factor(firsts[:, level // 2, :], z, level, 0)
                     else:
-                        for s in range(2 if level // 2 in (0, 1) else 1):
+                        for s in range(2 if level // 2 in (1,) else 1):
                             factor(pairs[:, level // 2, s, :], z, level, s)
 
                 steps.append(step)
@@ -331,7 +331,7 @@ def tile_neuralobliviousdecisiontree_e_kernel(tc, x, W_words, W_scales, b, leaf_
             firsts, pairs, cols = logs[first]
             planes = []
             for pair in range(DEPTH // 2):
-                if pair in (0, 1):
+                if pair in (1,):
                     planes.extend([pairs[:, pair, 0, :], pairs[:, pair, 1, :]])
                 else:
                     planes.extend([firsts[:, pair, :], pairs[:, pair, 0, :]])
@@ -356,7 +356,7 @@ def tile_neuralobliviousdecisiontree_e_kernel(tc, x, W_words, W_scales, b, leaf_
             firsts, pairs, cols = logs[t]
 
             def pair_sum(pair, bit, next_bit):
-                if pair in (0, 1):
+                if pair in (1,):
                     return [(pairs[:, pair, bit ^ next_bit, cols], swap if bit else ident)]
                 return [(firsts[:, pair, cols], swap if bit else ident), (pairs[:, pair, 0, cols], swap if next_bit else ident)]
 
@@ -389,8 +389,6 @@ def tile_neuralobliviousdecisiontree_e_kernel(tc, x, W_words, W_scales, b, leaf_
                             [P, PASSES, P, PACK], BF16, align_bytes=64, tag="log_path", bufs=LOG_PATHS, name="log_path"
                         )
                     bank = psum.tile([P, PACK, P], F32, tag="z" if g % 2 == 0 else "x_t")
-                    if g % 3 == 0:
-                        nc.tensor.matmul(out=bank[:, 0, 0:128], lhsT=ident[:], rhs=ident[:, 0:128], start=True, stop=True)
                     for j in range(PACK):
                         add_transposed(bank[:, j, :], [(sums[t][:, g, :], ident), (sums[t][:, PASSES + j, :], ident)])
                     nc.scalar.activation(out=paths[t][:, g, :, :], in_=bank[:].rearrange("p j n -> p n j"), func=EXP)
@@ -515,7 +513,7 @@ def tile_neuralobliviousdecisiontree_e_kernel(tc, x, W_words, W_scales, b, leaf_
         copy_lower(4)
         multiply(3)
         quantise_leaves()
-        for pair in (0, 1):
+        for pair in (1,):
             multiply_pairs(12, pair)
         do(logarithm_steps(12))
         work = []
@@ -532,7 +530,7 @@ def tile_neuralobliviousdecisiontree_e_kernel(tc, x, W_words, W_scales, b, leaf_
         weave(eights, work[0:4])
         for t in (0, 1, 2, 3):
             quantise(t)
-        runs = {4: [0, 1, 2, 3], 7: [4, 5, 6, 7], 10: [8, 9, 10, 12]}
+        runs = {7: [4, 5, 6, 7], 10: [8, 9, 10, 12]}
         done = 4
         for t in range(4, N_PRODUCT):
             multiply(t)
@@ -550,12 +548,13 @@ def tile_neuralobliviousdecisiontree_e_kernel(tc, x, W_words, W_scales, b, leaf_
                 prepare_a4(10, 2, nc.gpsimd)
                 prepare_a8(10, 1, nc.gpsimd)
                 prepare_a8(11, 1, nc.gpsimd)
+            if t in (4, 5):
+                for k in (2 * t - 8, 2 * t - 7):
+                    contract(k, k)
+                if t == 5:
+                    store([0, 1, 2, 3], 0, 4)
             if t in runs:
-                if t == 4:
-                    for place in range(4):
-                        contract(place, place)
-                else:
-                    do(finish_steps(runs[t]))
+                do(finish_steps(runs[t]))
                 store(runs[t], 0, 4)
         last = [13, 14, 15, 11]
         do(finish_steps(last))

from contextlib import ExitStack

import concourse.mybir as mybir
from concourse.masks import make_identity

F32 = mybir.dt.float32
BF16 = mybir.dt.bfloat16
I32 = mybir.dt.int32
U32 = mybir.dt.uint32
U8 = mybir.dt.uint8
FP8X4 = mybir.dt.float8_e4m3fn_x4
MULT = mybir.AluOpType.mult
SIGMOID = mybir.ActivationFunctionType.Sigmoid
LN = mybir.ActivationFunctionType.Ln
EXP = mybir.ActivationFunctionType.Exp
COPY = mybir.ActivationFunctionType.Copy

P = 128
PACK = 4
BATCH, FEATURES, DEPTH, TREES, LEAVES, D_OUT = 2048, 512, 6, 64, 64, 128
PASSES = TREES * LEAVES // (P * PACK)
N_TILES = BATCH // P
CHUNK_TILES = 4
CHUNK = CHUNK_TILES * P
N_CHUNKS = N_TILES // CHUNK_TILES
N_PRODUCT = 12
LEVEL_ORDER = (4, 5, 0, 1, 2, 3)
HALF_LEVELS = (0, 4)
LOG_PATHS = 4

FLOPS = 2 * BATCH * FEATURES * DEPTH * TREES + 2 * BATCH * TREES * LEAVES * D_OUT


def tile_neuralobliviousdecisiontree_e_kernel(tc, x, W_words, W_scales, b, leaf_values, out):
    nc = tc.nc
    with ExitStack() as ctx:
        ctx.enter_context(tc.manual_schedule())
        const = ctx.enter_context(tc.tile_pool(name="const", bufs=1))
        x_pool = ctx.enter_context(tc.tile_pool(name="x_pool", bufs=3))
        factor_pool = ctx.enter_context(tc.tile_pool(name="factor_pool", bufs=2))
        scratch_pool = ctx.enter_context(tc.tile_pool(name="scratch_pool", bufs=4))
        product_pool = ctx.enter_context(tc.tile_pool(name="product_pool", bufs=3))
        path_pool = ctx.enter_context(tc.tile_pool(name="path_pool", bufs=4))
        out_pool = ctx.enter_context(tc.tile_pool(name="out_pool", bufs=2))
        psum = ctx.enter_context(tc.psum_pool(name="psum", bufs=2))

        x_rows = x.rearrange("(p c) f -> p c f", c=N_TILES)
        out_rows = out.rearrange("(p c) d -> p c d", c=N_TILES)
        x_raw = []
        for q in range(N_CHUNKS):
            x_raw.append(scratch_pool.tile([P, CHUNK_TILES, FEATURES], BF16, tag="scratch", name="x_raw"))

        def load_x(q, lo, hi):
            nc.sync.dma_start(
                out=x_raw[q][:, lo:hi, :], in_=x_rows[:, q * CHUNK_TILES + lo : q * CHUNK_TILES + hi, :]
            )

        w_codes = const.tile([P, DEPTH, 2, TREES], U32, align_bytes=64)
        w_scales = const.tile([P, DEPTH, 2, TREES], U8, align_bytes=64)
        b_rows = const.tile([P, P], BF16)
        leaf_raw = path_pool.tile([P, LEAVES // 2, D_OUT], BF16, align_bytes=64, tag="log_path", bufs=LOG_PATHS, name="leaf_raw")
        nc.vector.memset(w_scales[:].rearrange("p j h t -> p (j h t)").bitcast(I32), 0)
        nc.vector.memset(b_rows[:], 0.0)
        for b0 in range(2):
            nc.scalar.dma_start(out=b_rows[0:DEPTH, TREES * b0 : TREES * (b0 + 1)], in_=b)
        load_x(0, 0, 2)
        nc.sync.dma_start(
            out=w_codes[:, :, 0, :].bitcast(I32),
            in_=W_words.rearrange("j p t e -> p j (t e)").bitcast(I32),
        )
        load_x(0, 2, 4)
        scale_rows = W_scales.rearrange("j s t -> s j t").bitcast(I32)
        for quadrant in range(4):
            nc.sync.dma_start(
                out=w_scales[32 * quadrant : 32 * quadrant + 4, :, 0, :].bitcast(I32),
                in_=scale_rows[4 * quadrant : 4 * quadrant + 4, :, :],
            )
        load_x(1, 0, 4)
        half_leaves = LEAVES // 2
        nc.sync.dma_start(out=leaf_raw[0:TREES, :, :], in_=leaf_values[:, 0:half_leaves, :])
        load_x(2, 0, 4)
        load_x(3, 0, 4)
        for k in range(half_leaves):
            nc.sync.dma_start(out=leaf_raw[TREES:P, k, :], in_=leaf_values[:, LEAVES - 1 - k, :])

        ident = const.tile([P, P], F32)
        make_identity(nc, ident[:])
        half_sign = const.tile([P, 2], F32)
        nc.vector.memset(half_sign[:], -1.0)
        nc.vector.memset(half_sign[0:TREES, 0:1], 1.0)
        nc.vector.memset(half_sign[TREES:P, 1:2], 1.0)
        floor = const.tile([P, 1], F32)
        nc.vector.memset(floor[:], 1e-30)
        table_warmer = const.tile([P, 1], F32)
        nc.scalar.activation(out=table_warmer[:], in_=half_sign[:, 0:1], func=SIGMOID)

        b_rows_f32 = const.tile([P, P], F32)
        nc.vector.tensor_copy(out=b_rows_f32[:], in_=b_rows[:])
        swap = const.tile([P, P], F32)
        nc.vector.tensor_copy(out=swap[:, 0:TREES], in_=ident[:, TREES:P])
        nc.vector.tensor_copy(out=swap[:, TREES:P], in_=ident[:, 0:TREES])
        nc.vector.tensor_copy(out=w_codes[:, :, 1, :].bitcast(I32), in_=w_codes[:, :, 0, :].bitcast(I32))
        nc.vector.tensor_copy(out=w_scales[:, :, 1, :].bitcast(I32), in_=w_scales[:, :, 0, :].bitcast(I32))

        leaf_grouped = path_pool.tile(
            [P, PASSES, D_OUT, PACK], BF16, align_bytes=64, tag="log_path", bufs=LOG_PATHS, name="leaf_grouped"
        )
        leaf_codes = const.tile([P, PASSES, D_OUT], U32, align_bytes=64)
        leaf_scales = const.tile([P, PASSES, D_OUT], U8, align_bytes=64)

        def regroup_leaves(lo, hi):
            nc.scalar.copy(
                out=leaf_grouped[:, lo:hi, :, :],
                in_=leaf_raw[:, PACK * lo : PACK * hi, :].rearrange("p (g j) d -> p g d j", j=PACK),
            )

        def quantise_leaves():
            nc.vector.quantize_mx(
                out=leaf_codes[:].rearrange("p g d -> p (g d)").bitcast(FP8X4),
                scales=leaf_scales[:].rearrange("p g d -> p (g d)"),
                in_=leaf_grouped[:].rearrange("p g d j -> p (g d j)"),
            )

        def do(step_list):
            for step in step_list:
                step()

        x_grouped = {}
        x_mx = {}

        def transpose_x(q, pair, eng_copy):
            x_words = x_raw[q][:].rearrange("p c f -> p (c f)").bitcast(F32)
            words_per_row = FEATURES // 2
            if pair == 0:
                x_grouped[q] = x_pool.tile([P, CHUNK * PACK], BF16, align_bytes=64, name="x_grouped")
            grouped_words = x_grouped[q][:].bitcast(F32).rearrange("p (c n u) -> p c n u", c=CHUNK_TILES, u=2)
            x_t = psum.tile([P, 2, 2, P], F32, tag="x_t")
            for i in range(2):
                first = (2 * pair + i) * words_per_row
                for u in range(2):
                    nc.tensor.transpose(
                        out=x_t[:, i, u, :],
                        in_=x_words[:, first + u : first + words_per_row : 2],
                        identity=ident[:],
                    )
            eng_copy(
                out=grouped_words[:, 2 * pair : 2 * pair + 2, :, :],
                in_=x_t[:].rearrange("p c u n -> p c n u"),
            )

        def quantise_x(q, lo, hi):
            if lo == 0:
                x_codes = const.tile([P, CHUNK], U32, align_bytes=64, name="x_codes%d" % q)
                x_scales = const.tile([P, CHUNK], U8, align_bytes=64, name="x_scales%d" % q)
                x_mx[q] = (x_codes, x_scales)
            cols = slice(lo * P, hi * P)
            nc.vector.quantize_mx(
                out=x_mx[q][0][:, cols].bitcast(FP8X4),
                scales=x_mx[q][1][:, cols],
                in_=x_grouped[q][:, PACK * lo * P : PACK * hi * P],
            )

        def logits(level, first, n):
            q, i = divmod(first, CHUNK_TILES)
            cols = slice(i * P, (i + n) * P)
            x_codes, x_scales = x_mx[q]
            z = psum.tile([P, CHUNK], F32, tag="z")
            nc.tensor.matmul_mx(
                out=z[:, 0 : n * P],
                lhsT=w_codes[:, level, :, :].rearrange("p h t -> p (h t)").bitcast(FP8X4),
                lhsT_scale=w_scales[:, level, :, :].rearrange("p h t -> p (h t)"),
                rhs=x_codes[:, cols].bitcast(FP8X4),
                rhs_scale=x_scales[:, cols],
                start=True,
                stop=True,
            )
            return z[:, 0 : n * P]

        def factor(out_ap, z, level, s):
            nc.scalar.activation(
                out=out_ap, in_=z, func=SIGMOID, bias=half_bias[:, s, level : level + 1], scale=half_sign[:, s : s + 1]
            )

        factors = {}

        def new_factor(q, level, bits):
            return factor_pool.tile([P, bits, CHUNK], F32, name="f%d" % level)

        def factor_steps(first, n):
            q, i = divmod(first, CHUNK_TILES)
            cols = slice(i * P, (i + n) * P)
            steps = []
            for level in LEVEL_ORDER:

                def step_0(level=level):
                    half = level in HALF_LEVELS
                    if (q, level) not in factors:
                        factors[(q, level)] = new_factor(q, level, 1 if half else 2)
                    zs[0] = logits(level, first, n)
                    factor(factors[(q, level)][:, 0, cols], zs[0], level, 0)

                def step_1(level=level):
                    factor(factors[(q, level)][:, 1, cols], zs[0], level, 1)

                steps.append(step_0)
                if level not in HALF_LEVELS:
                    steps.append(step_1)
            return steps

        upper = {}
        lower = {}

        def prepare_lower(t, n, eng):
            q, i = divmod(t, CHUNK_TILES)
            cols = slice(i * P, (i + n) * P)
            c2 = product_pool.tile([P, 2, CHUNK], F32, name="c2", bufs=2)
            eng.tensor_tensor(
                out=c2[:, :, 0 : n * P],
                in0=factors[(q, 4)][:, :, cols].to_broadcast([P, 2, n * P]),
                in1=factors[(q, 5)][:, :, cols],
                op=MULT,
            )
            for k in range(n):
                lower[t + k] = c2[:, :, k * P : (k + 1) * P]

        partial = {}

        def prepare_a2(t, n, eng):
            q, i = divmod(t, CHUNK_TILES)
            cols = slice(i * P, (i + n) * P)
            a2 = product_pool.tile([P, 2, CHUNK], F32, name="a2", bufs=1)
            eng.tensor_tensor(
                out=a2[:, :, 0 : n * P],
                in0=factors[(q, 0)][:, :, cols].to_broadcast([P, 2, n * P]),
                in1=factors[(q, 1)][:, :, cols],
                op=MULT,
            )
            for k in range(n):
                partial[("a2", t + k)] = (a2, k)

        def prepare_a4(t, n, eng):
            q, i = divmod(t, CHUNK_TILES)
            a2, k0 = partial[("a2", t)]
            a4 = product_pool.tile([P, 2, 2, 2 * P], F32, name="a4", bufs=1)
            eng.tensor_tensor(
                out=a4[:, :, :, 0 : n * P],
                in0=a2[:, :, k0 * P : (k0 + n) * P].unsqueeze(2).to_broadcast([P, 2, 2, n * P]),
                in1=factors[(q, 2)][:, :, i * P : (i + n) * P].unsqueeze(1).to_broadcast([P, 2, 2, n * P]),
                op=MULT,
            )
            for k in range(n):
                partial[("a4", t + k)] = (a4, k)

        def prepare_a8(t, n, eng):
            q, i = divmod(t, CHUNK_TILES)
            a4, k0 = partial[("a4", t)]
            a8 = product_pool.tile([P, 4, 2, 1 * P], F32, name="a8", bufs=3)
            eng.tensor_tensor(
                out=a8[:, :, :, 0 : n * P],
                in0=a4[:, :, :, k0 * P : (k0 + n) * P]
                .rearrange("p a b n -> p (a b) n")
                .unsqueeze(2)
                .to_broadcast([P, 4, 2, n * P]),
                in1=factors[(q, 3)][:, :, i * P : (i + n) * P].unsqueeze(1).to_broadcast([P, 4, 2, n * P]),
                op=MULT,
            )
            for k in range(n):
                upper[t + k] = a8[:].rearrange("p a b n -> p (a b) n")[:, :, k * P : (k + 1) * P]

        lower_banks = {}

        def copy_lower_steps(t):
            def step_0():
                lower_banks[t] = psum.tile([P, PACK, P], F32, tag="lower_ps", bufs=3, name="lower_ps")
                nc.tensor.matmul(out=lower_banks[t][:, 0:2, :], lhsT=ident[:], rhs=lower[t], start=True, stop=True)

            def step_1():
                for j in (2, 3):
                    nc.tensor.matmul(
                        out=lower_banks[t][:, j, :], lhsT=swap[:], rhs=lower[t][:, 3 - j, :], start=True, stop=True
                    )

            return [step_0, step_1]

        def copy_lower(t):
            do(copy_lower_steps(t))

        paths = {}

        def multiply(t):
            path = path_pool.tile([P, PASSES, P, PACK], BF16, align_bytes=64, name="path")
            nc.vector.tensor_tensor(
                out=path[:],
                in0=upper[t].unsqueeze(3).to_broadcast([P, PASSES, P, PACK]),
                in1=lower_banks[t][:].rearrange("p j n -> p n j").unsqueeze(1).to_broadcast([P, PASSES, P, PACK]),
                op=MULT,
            )
            paths[t] = path

        logs = {}

        def log_factor_steps(first, n):
            firsts = const.tile([P, DEPTH // 2, n * P], F32, name="log_firsts")
            pairs = const.tile([P, DEPTH // 2, 2, n * P], F32, name="log_pairs")
            for k in range(n):
                logs[first + k] = (firsts, pairs, slice(k * P, (k + 1) * P))
            steps = []
            for level in range(DEPTH):

                def step(level=level):
                    z = logits(level, first, n)
                    if level % 2 == 0:
                        factor(firsts[:, level // 2, :], z, level, 0)
                    else:
                        for s in range(2 if level // 2 in (1,) else 1):
                            factor(pairs[:, level // 2, s, :], z, level, s)

                steps.append(step)
            return steps

        def multiply_pairs(first, pair):
            firsts, pairs, cols = logs[first]
            nc.vector.tensor_tensor(
                out=pairs[:, pair, :, :],
                in0=firsts[:, pair : pair + 1, :].to_broadcast([P, 2, firsts.shape[2]]),
                in1=pairs[:, pair, :, :],
                op=MULT,
            )

        def logarithm_steps(first):
            firsts, pairs, cols = logs[first]
            planes = []
            for pair in range(DEPTH // 2):
                if pair in (1,):
                    planes.extend([pairs[:, pair, 0, :], pairs[:, pair, 1, :]])
                else:
                    planes.extend([firsts[:, pair, :], pairs[:, pair, 0, :]])
            steps = []
            for plane in planes:

                def step(plane=plane):
                    nc.scalar.activation(out=plane, in_=plane, func=LN, bias=floor[:])

                steps.append(step)
            return steps

        def add_transposed(out_ap, parts):
            for k, (part, matrix) in enumerate(parts):
                nc.tensor.matmul(
                    out=out_ap, lhsT=part, rhs=matrix[:], start=(k == 0), stop=(k == len(parts) - 1), is_transpose=True
                )

        sums = {}

        def sum_steps(t):
            firsts, pairs, cols = logs[t]

            def pair_sum(pair, bit, next_bit):
                if pair in (1,):
                    return [(pairs[:, pair, bit ^ next_bit, cols], swap if bit else ident)]
                return [(firsts[:, pair, cols], swap if bit else ident), (pairs[:, pair, 0, cols], swap if next_bit else ident)]

            steps = []
            for k0 in range(0, PASSES + PACK, PACK):

                def sum_step(k0=k0):
                    if k0 == 0:
                        sums[t] = scratch_pool.tile([P, PASSES + PACK, P], F32, tag="scratch", name="log_sums")
                    bank = psum.tile([P, 4, P], F32, tag="x_t")
                    for k in range(4):
                        if k0 < PASSES:
                            g = k0 + k
                            parts = pair_sum(0, 0, g >> 2) + pair_sum(1, (g >> 1) & 1, g & 1)
                        else:
                            parts = pair_sum(2, k >> 1, k & 1)
                        add_transposed(bank[:, k, :], parts)
                    nc.scalar.copy(out=sums[t][:, k0 : k0 + 4, :], in_=bank[:])

                steps.append(sum_step)
            return steps

        def exp_steps(t):
            steps = []
            for g in range(PASSES):

                def exp_step(g=g):
                    if g == 0:
                        paths[t] = path_pool.tile(
                            [P, PASSES, P, PACK], BF16, align_bytes=64, tag="log_path", bufs=LOG_PATHS, name="log_path"
                        )
                    bank = psum.tile([P, PACK, P], F32, tag="z" if g % 2 == 0 else "x_t")
                    for j in range(PACK):
                        add_transposed(bank[:, j, :], [(sums[t][:, g, :], ident), (sums[t][:, PASSES + j, :], ident)])
                    nc.scalar.activation(out=paths[t][:, g, :, :], in_=bank[:].rearrange("p j n -> p n j"), func=EXP)

                steps.append(exp_step)
            return steps

        codes = {}

        def quantise(t):
            path_codes = path_pool.tile([P, PASSES, P], U32, align_bytes=64, bufs=4, name="path_codes")
            path_scales = path_pool.tile([P, PASSES, P], U8, align_bytes=64, bufs=4, name="path_scales")
            nc.vector.quantize_mx(
                out=path_codes[:].rearrange("p g n -> p (g n)").bitcast(FP8X4),
                scales=path_scales[:].rearrange("p g n -> p (g n)"),
                in_=paths[t][:].rearrange("p g n j -> p (g n j)"),
            )
            codes[t] = (path_codes, path_scales)

        accs = []

        def contract(t, place):
            path_codes, path_scales = codes[t]
            if place == 0:
                accs.append(psum.tile([P, CHUNK_TILES, D_OUT], F32, tag="acc", bufs=1, name="acc"))
            for g in range(PASSES):
                nc.tensor.matmul_mx(
                    out=accs[-1][:, place, :],
                    lhsT=path_codes[:, g, :].bitcast(FP8X4),
                    lhsT_scale=path_scales[:, g, :],
                    rhs=leaf_codes[:, g, :].bitcast(FP8X4),
                    rhs_scale=leaf_scales[:, g, :],
                    start=(g == 0),
                    stop=(g == PASSES - 1),
                )

        def store(run, lo, hi):
            result = out_pool.tile([P, CHUNK_TILES, D_OUT], F32, name="result")
            nc.scalar.activation(out=result[:, lo:hi, :], in_=accs[-1][:, lo:hi, :], func=COPY, scale=1.0 / TREES)
            for place in range(lo, hi):
                nc.sync.dma_start(out=out_rows[:, run[place], :], in_=result[:, place, :])

        zs = [None]

        for k in range(4):
            warm = psum.tile([P, P], F32, tag="z")
            nc.tensor.matmul(out=warm[:], lhsT=ident[:], rhs=ident[:], start=True, stop=True)
        b_cols = psum.tile([P, P], F32, tag="x_t")
        nc.tensor.transpose(out=b_cols[:], in_=b_rows_f32[:], identity=ident[:])
        half_bias = const.tile([P, 2, DEPTH], F32)
        for s in range(2):
            nc.vector.tensor_scalar_mul(out=half_bias[:, s, :], in0=b_cols[:, 0:DEPTH], scalar1=half_sign[:, s : s + 1])
        transpose_x(0, 0, nc.scalar.copy)
        quantise_x(0, 0, 2)
        def weave(*step_lists):
            marked = []
            for n, step_list in enumerate(step_lists):
                for k, step in enumerate(step_list):
                    marked.append(((k + 0.5) / len(step_list), n, k, step))
            for mark in sorted(marked, key=lambda mark: mark[0:3]):
                mark[3]()

        def finish_steps(run):
            steps = []
            for place, t in enumerate(run):

                def step(place=place, t=t):
                    quantise(t)
                    contract(t, place)

                steps.append(step)
            return steps

        firsts = factor_steps(0, 2)
        do(firsts[0:3])
        prepare_lower(0, 2, nc.vector)
        transpose_x(0, 1, nc.vector.tensor_copy)
        quantise_x(0, 2, 4)
        do(firsts[3:])
        prepare_a2(0, 2, nc.vector)
        prepare_a4(0, 2, nc.vector)
        prepare_a8(0, 1, nc.vector)
        copy_lower(0)
        prepare_a8(1, 1, nc.gpsimd)
        seconds = factor_steps(2, 2)
        do(seconds[0:3])
        copy_lower(1)
        prepare_lower(2, 2, nc.gpsimd)
        do(seconds[3:])
        for pair in range(2):
            transpose_x(1, pair, nc.scalar.copy)
        regroup_leaves(0, 4)
        multiply(0)
        quantise_x(1, 0, 4)
        prepare_a2(2, 2, nc.gpsimd)
        prepare_a4(2, 2, nc.gpsimd)
        for t in (2, 3):
            prepare_a8(t, 1, nc.gpsimd)
        later_x = []
        for q in (3, 2):
            for pair in range(2):
                later_x.append(lambda q=q, pair=pair: transpose_x(q, pair, nc.scalar.copy))
        fours = factor_steps(4, 4)
        copy_lower(2)
        weave(fours[0:5], later_x[0:2])
        weave(fours[5:], later_x[2:4])
        prepare_lower(4, 4, nc.gpsimd)
        prepare_a2(4, 4, nc.gpsimd)
        prepare_a4(4, 2, nc.gpsimd)
        prepare_a8(4, 1, nc.gpsimd)
        prepare_a8(5, 1, nc.gpsimd)
        prepare_a4(6, 2, nc.gpsimd)
        prepare_a8(6, 1, nc.gpsimd)
        prepare_a8(7, 1, nc.gpsimd)
        multiply(1)
        regroup_leaves(4, 8)
        copy_lower(3)
        multiply(2)
        quantise_x(3, 0, 4)
        quantise_x(2, 0, 4)
        do(log_factor_steps(12, 4))
        copy_lower(4)
        multiply(3)
        quantise_leaves()
        for pair in (1,):
            multiply_pairs(12, pair)
        do(logarithm_steps(12))
        work = []
        for t in (12, 13):
            work.extend(sum_steps(t))
        work.extend(exp_steps(12))
        work.extend(sum_steps(14))
        work.extend(exp_steps(13))
        work.extend(sum_steps(15))
        work.extend(exp_steps(14))
        work.extend(exp_steps(15))
        eights = factor_steps(8, 4)
        copy_lower(5)
        weave(eights, work[0:4])
        for t in (0, 1, 2, 3):
            quantise(t)
        runs = {7: [4, 5, 6, 7], 10: [8, 9, 10, 12]}
        done = 4
        for t in range(4, N_PRODUCT):
            multiply(t)
            if t + 2 < N_PRODUCT:
                copy_lower(t + 2)
            upto = 4 + (len(work) - 4) * min(t - 3, 7) // 7
            do(work[done:upto])
            done = upto
            if t == 5:
                prepare_lower(8, 4, nc.gpsimd)
                prepare_a2(8, 4, nc.gpsimd)
                prepare_a4(8, 2, nc.gpsimd)
                prepare_a8(8, 1, nc.gpsimd)
                prepare_a8(9, 1, nc.gpsimd)
                prepare_a4(10, 2, nc.gpsimd)
                prepare_a8(10, 1, nc.gpsimd)
                prepare_a8(11, 1, nc.gpsimd)
            if t in (4, 5):
                for k in (2 * t - 8, 2 * t - 7):
                    contract(k, k)
                if t == 5:
                    store([0, 1, 2, 3], 0, 4)
            if t in runs:
                do(finish_steps(runs[t]))
                store(runs[t], 0, 4)
        last = [13, 14, 15, 11]
        do(finish_steps(last))
        store(last, 0, 3)
        store(last, 3, 4)
